import numpy as np
import ml_dtypes


def mxq(x, axis, fmt="e4m3"):
    dtype, down = {"e4m3": (ml_dtypes.float8_e4m3fn, 7), "e5m2": (ml_dtypes.float8_e5m2, 14)}[fmt]
    v = np.moveaxis(np.asarray(x, np.float32).astype(ml_dtypes.bfloat16).astype(np.float64), axis, -1)
    blocks = v.reshape(v.shape[:-1] + (-1, 32))
    amax = np.abs(blocks).max(-1, keepdims=True)
    byte = np.maximum(np.where(amax > 0, np.frexp(amax)[1] - 1 + 127, 0) - down, 1)
    scale = np.exp2(byte - 127.0)
    codes = (blocks / scale).astype(np.float32).astype(dtype).astype(np.float64)
    return np.moveaxis((codes * scale).reshape(v.shape), -1, axis)


WIDE = False


def mx_kscale(k):
    if not WIDE:
        return np.ones(k)
    levels = np.array([10, -10, 5, -5, 0])
    a = np.random.permutation(np.resize(levels, k // 512 * 4)).reshape(k // 512, 4)
    idx = np.arange(k)
    return np.exp2(a[idx // 512, idx % 128 // 32])


BF16 = ml_dtypes.bfloat16


def bf(x):
    return np.asarray(x, np.float32).astype(BF16)


def f64(x):
    return np.asarray(x).astype(np.float64)


B, F, M, N, H, O = 1, 128, 128, 128, 512, 128
BN_EPS = 1e-5


def bn(x, g, b, m, v):
    sh = [1] * x.ndim
    sh[1] = -1
    return g.reshape(sh) * (x - m.reshape(sh)) * (1.0 / np.sqrt(v.reshape(sh) + BN_EPS)) + b.reshape(sh)


def setup_inputs():
    s = mx_kscale(H)
    k = mx_kscale(H)
    return {"h2": bf(np.maximum(np.random.standard_normal((B, H, M, N)), 0.0) * s[None, :, None, None]),
            "W3": bf(np.random.standard_normal((H, H)) * 1.4 / np.sqrt(H) / s[None, :]),
            "g3": bf((1.0 + 0.1 * np.random.standard_normal(H)) * k),
            "b3": bf(0.2 * np.random.standard_normal(H) * k),
            "m3": bf(0.2 * np.random.standard_normal(H)),
            "v3": bf(np.random.uniform(0.5, 1.5, H)),
            "Wc1": bf(np.random.standard_normal((H, H)) * 0.4 / np.sqrt(H) / k[None, :]),
            "gc1": bf(1.0 + 0.1 * np.random.standard_normal(H)),
            "bc1": bf(0.2 * np.random.standard_normal(H)),
            "mc1": bf(0.2 * np.random.standard_normal(H)),
            "vc1": bf(np.random.uniform(0.5, 1.5, H))}


def reference(h2, W3, g3, b3, m3, v3, Wc1, gc1, bc1, mc1, vc1):
    x3 = (mxq(f64(W3), 1, "e4m3") @ mxq(f64(h2).reshape(B, H, M * N), 1, "e4m3")).reshape(B, H, M, N)
    h3 = np.maximum(bn(x3, f64(g3), f64(b3), f64(m3), f64(v3)), 0.0)
    p = h3.max(axis=2)
    xc = mxq(f64(Wc1), 1, "e4m3") @ mxq(p, 1, "e4m3")
    return np.maximum(bn(xc, f64(gc1), f64(bc1), f64(mc1), f64(vc1)), 0.0)

@@ -1,0 +1,180 @@
+import concourse.mybir as mybir
+from concourse.masks import make_identity
+
+FLOPS = 2 * 512 * 512 * (128 * 128) + 2 * 512 * 512 * 128
+
+BF16 = mybir.dt.bfloat16
+F32 = mybir.dt.float32
+U32 = mybir.dt.uint32
+U8 = mybir.dt.uint8
+FP8X4 = mybir.dt.float8_e4m3fn_x4
+RELU = mybir.ActivationFunctionType.Relu
+
+P = 128
+PACK = 4
+H = P * PACK
+PAIRS = 128 * 128
+N_SEARCH = 128
+COLS = 512
+PIECES = PAIRS // COLS
+RUN = 4
+SCALAR_COLS = 64
+RAW_BUFS = 6
+BN_EPS = 1e-5
+
+
+def tile_p2b_xcorr_pb_kernel(tc, h2, W3, g3, b3, m3, v3, Wc1, gc1, bc1, mc1, vc1, out):
+    nc = tc.nc
+    h2_rows = h2[0].rearrange("(p j) m n -> p j (m n)", j=PACK)
+
+    with (
+        tc.tile_pool(name="const", bufs=1) as const,
+        tc.tile_pool(name="raw", bufs=RAW_BUFS) as raw_pool,
+        tc.tile_pool(name="work", bufs=3) as work,
+        tc.psum_pool(name="banks", bufs=6) as banks,
+        tc.psum_pool(name="side", bufs=2) as side,
+    ):
+        raw = {}
+        grouped = {}
+        codes = {}
+        scales = {}
+        h3 = {}
+
+        def load(i):
+            raw[i] = raw_pool.tile([P, PACK, COLS], BF16, name="raw")
+            nc.sync.dma_start(out=raw[i][:], in_=h2_rows[:, :, i * COLS : (i + 1) * COLS])
+
+        def regroup(i):
+            grouped[i] = work.tile([P, COLS, PACK], BF16, name="grouped", align_bytes=64)
+            dst = grouped[i][:].rearrange("p (c r) j -> p c j r", r=RUN)
+            src = raw[i][:].rearrange("p j (c r) -> p c j r", r=RUN)
+            cut = (COLS - SCALAR_COLS) // RUN
+            nc.vector.tensor_copy(out=dst[:, :cut], in_=src[:, :cut])
+            nc.scalar.copy(out=dst[:, cut:], in_=src[:, cut:])
+
+        def quantise(i):
+            codes[i] = work.tile([P, COLS], U32, name="codes", align_bytes=64)
+            scales[i] = work.tile([P, COLS], U8, name="scales", align_bytes=64)
+            nc.vector.quantize_mx(
+                out=codes[i][:].bitcast(FP8X4),
+                scales=scales[i][:],
+                in_=grouped[i][:].rearrange("p w j -> p (w j)"),
+            )
+
+        def prepare_weight(w, label):
+            w_sb = const.tile([P, PACK, H], BF16, name=label + "_sb")
+            nc.sync.dma_start(out=w_sb[:], in_=w.rearrange("(q t) h -> q t h", t=PACK))
+            w_codes = const.tile([P, PACK, P], U32, name=label + "_codes", align_bytes=64)
+            w_scales = const.tile([P, PACK, P], U8, name=label + "_scales", align_bytes=64)
+            for t in range(PACK):
+                words = w_sb[:, t, :].bitcast(F32).rearrange("q (p u) -> q u p", u=2)
+                turned = side.tile([P, 2, P], F32, name="turned", tag="side")
+                for u in range(2):
+                    nc.tensor.transpose(turned[:, u, :], words[:, u, :], identity[:])
+                w_grouped = work.tile([P, H], BF16, name="w_grouped", align_bytes=64)
+                nc.scalar.copy(
+                    out=w_grouped[:].bitcast(F32).rearrange("p (q u) -> p q u", u=2),
+                    in_=turned[:].rearrange("p u q -> p q u"),
+                )
+                nc.vector.quantize_mx(
+                    out=w_codes[:, t, :].bitcast(FP8X4), scales=w_scales[:, t, :], in_=w_grouped[:]
+                )
+            return w_codes, w_scales
+
+        def batch_norm_affine(g, b, m, v, label):
+            loaded = const.tile([P, 4, 16], BF16, name=label + "_loaded")
+            for slot, vec in enumerate((g, b, m, v)):
+                nc.scalar.dma_start(out=loaded[:, slot, 0:PACK], in_=vec.rearrange("(q t) -> q t", t=PACK))
+            spread = const.tile([P, PACK], F32, name=label + "_spread")
+            gain = const.tile([P, PACK], F32, name=label + "_gain")
+            offset = const.tile([P, PACK], F32, name=label + "_offset")
+            shift = const.tile([P, PACK], F32, name=label + "_shift")
+            nc.vector.tensor_scalar_add(out=spread[:], in0=loaded[:, 3, 0:PACK], scalar1=BN_EPS)
+            nc.scalar.sqrt(out=spread[:], in_=spread[:])
+            nc.vector.reciprocal(out=spread[:], in_=spread[:])
+            nc.vector.tensor_mul(out=gain[:], in0=loaded[:, 0, 0:PACK], in1=spread[:])
+            nc.vector.tensor_mul(out=offset[:], in0=gain[:], in1=loaded[:, 2, 0:PACK])
+            nc.vector.tensor_sub(out=shift[:], in0=loaded[:, 1, 0:PACK], in1=offset[:])
+            return gain, shift
+
+        def multiply(i):
+            h3[i] = best if i == 0 else work.tile([P, PACK, COLS], BF16, name="h3")
+            for t in range(PACK):
+                x3 = banks.tile([P, COLS], F32, name="x3")
+                nc.tensor.matmul_mx(
+                    out=x3[:],
+                    lhsT=w3_codes[:, t, :].bitcast(FP8X4),
+                    lhsT_scale=w3_scales[:, t, :],
+                    rhs=codes[i][:].bitcast(FP8X4),
+                    rhs_scale=scales[i][:],
+                    start=True,
+                    stop=True,
+                )
+                nc.scalar.activation(
+                    out=h3[i][:, t, :], in_=x3[:], func=RELU, bias=shift1[:, t : t + 1], scale=gain1[:, t : t + 1]
+                )
+
+        def merge(i):
+            nc.vector.tensor_max(out=best[:], in0=best[:], in1=h3[i][:])
+
+        warm = const.tile([P, 1], F32, name="warm")
+        nc.vector.memset(warm[:], 1.0)
+        nc.scalar.sqrt(out=warm[:], in_=warm[:])
+        identity = const.tile([P, P], F32, name="identity")
+        make_identity(nc, identity[:])
+        best = const.tile([P, PACK, COLS], BF16, name="best")
+
+        load(0)
+        gain1, shift1 = batch_norm_affine(g3, b3, m3, v3, "bn1")
+        regroup(0)
+        quantise(0)
+        w3_codes, w3_scales = prepare_weight(W3, "w3")
+        for i in range(1, RAW_BUFS):
+            load(i)
+        regroup(1)
+
+        for i in range(PIECES):
+            multiply(i)
+            if i + 2 < PIECES:
+                regroup(i + 2)
+            if i + RAW_BUFS < PIECES:
+                load(i + RAW_BUFS)
+            if i + 1 < PIECES:
+                quantise(i + 1)
+            if i == 0:
+                wc_codes, wc_scales = prepare_weight(Wc1, "wc")
+                gain2, shift2 = batch_norm_affine(gc1, bc1, mc1, vc1, "bn2")
+            if i >= 2:
+                merge(i - 1)
+        merge(PIECES - 1)
+
+        half = const.tile([P, PACK, 2 * N_SEARCH], BF16, name="half")
+        nc.vector.tensor_max(out=half[:], in0=best[:, :, : 2 * N_SEARCH], in1=best[:, :, 2 * N_SEARCH :])
+        pooled = const.tile([P, N_SEARCH, PACK], BF16, name="pooled", align_bytes=64)
+        nc.vector.tensor_max(
+            out=pooled[:],
+            in0=half[:, :, :N_SEARCH].rearrange("p t n -> p n t"),
+            in1=half[:, :, N_SEARCH:].rearrange("p t n -> p n t"),
+        )
+        p_codes = const.tile([P, N_SEARCH], U32, name="p_codes", align_bytes=64)
+        p_scales = const.tile([P, N_SEARCH], U8, name="p_scales", align_bytes=64)
+        nc.vector.quantize_mx(
+            out=p_codes[:].bitcast(FP8X4), scales=p_scales[:], in_=pooled[:].rearrange("p n t -> p (n t)")
+        )
+        xc = side.tile([P, PACK, N_SEARCH], F32, name="xc", tag="side")
+        result = const.tile([P, PACK, N_SEARCH], F32, name="result")
+        for t in range(PACK):
+            nc.tensor.matmul_mx(
+                out=xc[:, t, :],
+                lhsT=wc_codes[:, t, :].bitcast(FP8X4),
+                lhsT_scale=wc_scales[:, t, :],
+                rhs=p_codes[:].bitcast(FP8X4),
+                rhs_scale=p_scales[:],
+                start=True,
+                stop=True,
+            )
+        for t in range(PACK):
+            nc.scalar.activation(
+                out=result[:, t, :], in_=xc[:, t, :], func=RELU, bias=shift2[:, t : t + 1], scale=gain2[:, t : t + 1]
+            )
+        nc.sync.dma_start(out=out[0].rearrange("(q t) n -> q t n", t=PACK), in_=result[:])

@@ -9,6 +9,8 @@ U32 = mybir.dt.uint32
 U8 = mybir.dt.uint8
 FP8X4 = mybir.dt.float8_e4m3fn_x4
 RELU = mybir.ActivationFunctionType.Relu
+MULT = mybir.AluOpType.mult
+ADD = mybir.AluOpType.add
 
 P = 128
 PACK = 4
@@ -51,6 +53,8 @@ def tile_p2b_xcorr_pb_kernel(tc, h2, W3, g3, b3, m3, v3, Wc1, gc1, bc1, mc1, vc1
             cut = (COLS - SCALAR_COLS) // RUN
             nc.vector.tensor_copy(out=dst[:, :cut], in_=src[:, :cut])
             nc.scalar.copy(out=dst[:, cut:], in_=src[:, cut:])
+            if i + RAW_BUFS < PIECES:
+                load(i + RAW_BUFS)
 
         def quantise(i):
             codes[i] = work.tile([P, COLS], U32, name="codes", align_bytes=64)
@@ -61,9 +65,12 @@ def tile_p2b_xcorr_pb_kernel(tc, h2, W3, g3, b3, m3, v3, Wc1, gc1, bc1, mc1, vc1
                 in_=grouped[i][:].rearrange("p w j -> p (w j)"),
             )
 
-        def prepare_weight(w, label):
+        def load_weight(w, label):
             w_sb = const.tile([P, PACK, H], BF16, name=label + "_sb")
             nc.sync.dma_start(out=w_sb[:], in_=w.rearrange("(q t) h -> q t h", t=PACK))
+            return w_sb
+
+        def quantise_weight(w_sb, label):
             w_codes = const.tile([P, PACK, P], U32, name=label + "_codes", align_bytes=64)
             w_scales = const.tile([P, PACK, P], U8, name=label + "_scales", align_bytes=64)
             for t in range(PACK):
@@ -81,20 +88,24 @@ def tile_p2b_xcorr_pb_kernel(tc, h2, W3, g3, b3, m3, v3, Wc1, gc1, bc1, mc1, vc1
                 )
             return w_codes, w_scales
 
-        def batch_norm_affine(g, b, m, v, label):
+        def load_batch_norm(g, b, m, v, label):
             loaded = const.tile([P, 4, 16], BF16, name=label + "_loaded")
             for slot, vec in enumerate((g, b, m, v)):
-                nc.scalar.dma_start(out=loaded[:, slot, 0:PACK], in_=vec.rearrange("(q t) -> q t", t=PACK))
+                nc.sync.dma_start(out=loaded[:, slot, 0:PACK], in_=vec.rearrange("(q t) -> q t", t=PACK))
+            return loaded
+
+        def batch_norm_affine(loaded, label):
+            g, b, m, v = (loaded[:, slot, 0:PACK] for slot in range(4))
             spread = const.tile([P, PACK], F32, name=label + "_spread")
             gain = const.tile([P, PACK], F32, name=label + "_gain")
             offset = const.tile([P, PACK], F32, name=label + "_offset")
             shift = const.tile([P, PACK], F32, name=label + "_shift")
-            nc.vector.tensor_scalar_add(out=spread[:], in0=loaded[:, 3, 0:PACK], scalar1=BN_EPS)
+            nc.vector.tensor_scalar_add(out=spread[:], in0=v, scalar1=BN_EPS)
             nc.scalar.sqrt(out=spread[:], in_=spread[:])
             nc.vector.reciprocal(out=spread[:], in_=spread[:])
-            nc.vector.tensor_mul(out=gain[:], in0=loaded[:, 0, 0:PACK], in1=spread[:])
-            nc.vector.tensor_mul(out=offset[:], in0=gain[:], in1=loaded[:, 2, 0:PACK])
-            nc.vector.tensor_sub(out=shift[:], in0=loaded[:, 1, 0:PACK], in1=offset[:])
+            nc.vector.tensor_mul(out=gain[:], in0=g, in1=spread[:])
+            nc.vector.tensor_mul(out=offset[:], in0=gain[:], in1=m)
+            nc.vector.tensor_sub(out=shift[:], in0=b, in1=offset[:])
             return gain, shift
 
         def multiply(i):
@@ -110,12 +121,39 @@ def tile_p2b_xcorr_pb_kernel(tc, h2, W3, g3, b3, m3, v3, Wc1, gc1, bc1, mc1, vc1
                     start=True,
                     stop=True,
                 )
-                nc.scalar.activation(
-                    out=h3[i][:, t, :], in_=x3[:], func=RELU, bias=shift1[:, t : t + 1], scale=gain1[:, t : t + 1]
-                )
+                if i == PIECES - 1 and t >= PACK // 2:
+                    nc.vector.tensor_scalar(
+                        out=h3[i][:, t, :],
+                        in0=x3[:],
+                        scalar1=gain1[:, t : t + 1],
+                        scalar2=shift1[:, t : t + 1],
+                        op0=MULT,
+                        op1=ADD,
+                    )
+                else:
+                    nc.scalar.activation(
+                        out=h3[i][:, t, :], in_=x3[:], func=RELU, bias=shift1[:, t : t + 1], scale=gain1[:, t : t + 1]
+                    )
 
         def merge(i):
             nc.vector.tensor_max(out=best[:], in0=best[:], in1=h3[i][:])
+
+        def fold(x, label):
+            two = const.tile([P, PACK, 2 * N_SEARCH], BF16, name=label + "_two")
+            one = const.tile([P, PACK, N_SEARCH], BF16, name=label + "_one")
+            nc.vector.tensor_max(out=two[:], in0=x[:, :, : 2 * N_SEARCH], in1=x[:, :, 2 * N_SEARCH :])
+            nc.vector.tensor_max(out=one[:], in0=two[:, :, :N_SEARCH], in1=two[:, :, N_SEARCH:])
+            return one
+
+        load(0)
+        bn1_loaded = load_batch_norm(g3, b3, m3, v3, "bn1")
+        w3_sb = load_weight(W3, "w3")
+        load(1)
+        load(2)
+        wc_sb = load_weight(Wc1, "wc")
+        bn2_loaded = load_batch_norm(gc1, bc1, mc1, vc1, "bn2")
+        for i in range(3, RAW_BUFS):
+            load(i)
 
         warm = const.tile([P, 1], F32, name="warm")
         nc.vector.memset(warm[:], 1.0)
@@ -124,57 +162,49 @@ def tile_p2b_xcorr_pb_kernel(tc, h2, W3, g3, b3, m3, v3, Wc1, gc1, bc1, mc1, vc1
         make_identity(nc, identity[:])
         best = const.tile([P, PACK, COLS], BF16, name="best")
 
-        load(0)
-        gain1, shift1 = batch_norm_affine(g3, b3, m3, v3, "bn1")
         regroup(0)
         quantise(0)
-        w3_codes, w3_scales = prepare_weight(W3, "w3")
-        for i in range(1, RAW_BUFS):
-            load(i)
+        gain1, shift1 = batch_norm_affine(bn1_loaded, "bn1")
+        w3_codes, w3_scales = quantise_weight(w3_sb, "w3")
         regroup(1)
+        gain2, shift2 = batch_norm_affine(bn2_loaded, "bn2")
+        wc_codes, wc_scales = quantise_weight(wc_sb, "wc")
 
-        for i in range(PIECES):
-            multiply(i)
-            if i + 2 < PIECES:
-                regroup(i + 2)
-            if i + RAW_BUFS < PIECES:
-                load(i + RAW_BUFS)
-            if i + 1 < PIECES:
-                quantise(i + 1)
-            if i == 0:
-                wc_codes, wc_scales = prepare_weight(Wc1, "wc")
-                gain2, shift2 = batch_norm_affine(gc1, bc1, mc1, vc1, "bn2")
-            if i >= 2:
-                merge(i - 1)
-        merge(PIECES - 1)
+        with tc.manual_schedule():
+            for i in range(PIECES):
+                if i + 1 < PIECES:
+                    quantise(i + 1)
+                if i + 2 < PIECES:
+                    regroup(i + 2)
+                multiply(i)
+                if i >= 2:
+                    merge(i - 1)
 
-        half = const.tile([P, PACK, 2 * N_SEARCH], BF16, name="half")
-        nc.vector.tensor_max(out=half[:], in0=best[:, :, : 2 * N_SEARCH], in1=best[:, :, 2 * N_SEARCH :])
-        pooled = const.tile([P, N_SEARCH, PACK], BF16, name="pooled", align_bytes=64)
-        nc.vector.tensor_max(
-            out=pooled[:],
-            in0=half[:, :, :N_SEARCH].rearrange("p t n -> p n t"),
-            in1=half[:, :, N_SEARCH:].rearrange("p t n -> p n t"),
-        )
-        p_codes = const.tile([P, N_SEARCH], U32, name="p_codes", align_bytes=64)
-        p_scales = const.tile([P, N_SEARCH], U8, name="p_scales", align_bytes=64)
-        nc.vector.quantize_mx(
-            out=p_codes[:].bitcast(FP8X4), scales=p_scales[:], in_=pooled[:].rearrange("p n t -> p (n t)")
-        )
-        xc = side.tile([P, PACK, N_SEARCH], F32, name="xc", tag="side")
-        result = const.tile([P, PACK, N_SEARCH], F32, name="result")
-        for t in range(PACK):
-            nc.tensor.matmul_mx(
-                out=xc[:, t, :],
-                lhsT=wc_codes[:, t, :].bitcast(FP8X4),
-                lhsT_scale=wc_scales[:, t, :],
-                rhs=p_codes[:].bitcast(FP8X4),
-                rhs_scale=p_scales[:],
-                start=True,
-                stop=True,
+            earlier = fold(best, "earlier")
+            last = fold(h3[PIECES - 1], "last")
+            pooled = const.tile([P, N_SEARCH, PACK], BF16, name="pooled", align_bytes=64)
+            nc.vector.tensor_max(
+                out=pooled[:], in0=earlier[:].rearrange("p t n -> p n t"), in1=last[:].rearrange("p t n -> p n t")
             )
-        for t in range(PACK):
-            nc.scalar.activation(
-                out=result[:, t, :], in_=xc[:, t, :], func=RELU, bias=shift2[:, t : t + 1], scale=gain2[:, t : t + 1]
+            p_codes = const.tile([P, N_SEARCH], U32, name="p_codes", align_bytes=64)
+            p_scales = const.tile([P, N_SEARCH], U8, name="p_scales", align_bytes=64)
+            nc.vector.quantize_mx(
+                out=p_codes[:].bitcast(FP8X4), scales=p_scales[:], in_=pooled[:].rearrange("p n t -> p (n t)")
             )
-        nc.sync.dma_start(out=out[0].rearrange("(q t) n -> q t n", t=PACK), in_=result[:])
+            xc = side.tile([P, PACK, N_SEARCH], F32, name="xc", tag="side")
+            result = const.tile([P, PACK, N_SEARCH], F32, name="result")
+            for t in range(PACK):
+                nc.tensor.matmul_mx(
+                    out=xc[:, t, :],
+                    lhsT=wc_codes[:, t, :].bitcast(FP8X4),
+                    lhsT_scale=wc_scales[:, t, :],
+                    rhs=p_codes[:].bitcast(FP8X4),
+                    rhs_scale=p_scales[:],
+                    start=True,
+                    stop=True,
+                )
+            for t in range(PACK):
+                nc.scalar.activation(
+                    out=result[:, t, :], in_=xc[:, t, :], func=RELU, bias=shift2[:, t : t + 1], scale=gain2[:, t : t + 1]
+                )
+            nc.sync.dma_start(out=out[0].rearrange("(q t) n -> q t n", t=PACK), in_=result[:])

@@ -9,8 +9,6 @@ U32 = mybir.dt.uint32
 U8 = mybir.dt.uint8
 FP8X4 = mybir.dt.float8_e4m3fn_x4
 RELU = mybir.ActivationFunctionType.Relu
-MULT = mybir.AluOpType.mult
-ADD = mybir.AluOpType.add
 
 P = 128
 PACK = 4
@@ -32,7 +30,8 @@ def tile_p2b_xcorr_pb_kernel(tc, h2, W3, g3, b3, m3, v3, Wc1, gc1, bc1, mc1, vc1
     with (
         tc.tile_pool(name="const", bufs=1) as const,
         tc.tile_pool(name="raw", bufs=RAW_BUFS) as raw_pool,
-        tc.tile_pool(name="work", bufs=3) as work,
+        tc.tile_pool(name="work", bufs=4) as work,
+        tc.tile_pool(name="packed", bufs=PIECES) as packed,
         tc.psum_pool(name="banks", bufs=6) as banks,
         tc.psum_pool(name="side", bufs=2) as side,
     ):
@@ -53,24 +52,19 @@ def tile_p2b_xcorr_pb_kernel(tc, h2, W3, g3, b3, m3, v3, Wc1, gc1, bc1, mc1, vc1
             cut = (COLS - SCALAR_COLS) // RUN
             nc.vector.tensor_copy(out=dst[:, :cut], in_=src[:, :cut])
             nc.scalar.copy(out=dst[:, cut:], in_=src[:, cut:])
-            if i + RAW_BUFS < PIECES:
-                load(i + RAW_BUFS)
 
         def quantise(i):
-            codes[i] = work.tile([P, COLS], U32, name="codes", align_bytes=64)
-            scales[i] = work.tile([P, COLS], U8, name="scales", align_bytes=64)
+            codes[i] = packed.tile([P, COLS], U32, name="codes", align_bytes=64)
+            scales[i] = packed.tile([P, COLS], U8, name="scales", align_bytes=64)
             nc.vector.quantize_mx(
                 out=codes[i][:].bitcast(FP8X4),
                 scales=scales[i][:],
                 in_=grouped[i][:].rearrange("p w j -> p (w j)"),
             )
 
-        def load_weight(w, label):
+        def prepare_weight(w, label):
             w_sb = const.tile([P, PACK, H], BF16, name=label + "_sb")
             nc.sync.dma_start(out=w_sb[:], in_=w.rearrange("(q t) h -> q t h", t=PACK))
-            return w_sb
-
-        def quantise_weight(w_sb, label):
             w_codes = const.tile([P, PACK, P], U32, name=label + "_codes", align_bytes=64)
             w_scales = const.tile([P, PACK, P], U8, name=label + "_scales", align_bytes=64)
             for t in range(PACK):
@@ -88,24 +82,20 @@ def tile_p2b_xcorr_pb_kernel(tc, h2, W3, g3, b3, m3, v3, Wc1, gc1, bc1, mc1, vc1
                 )
             return w_codes, w_scales
 
-        def load_batch_norm(g, b, m, v, label):
+        def batch_norm_affine(g, b, m, v, label):
             loaded = const.tile([P, 4, 16], BF16, name=label + "_loaded")
             for slot, vec in enumerate((g, b, m, v)):
-                nc.sync.dma_start(out=loaded[:, slot, 0:PACK], in_=vec.rearrange("(q t) -> q t", t=PACK))
-            return loaded
-
-        def batch_norm_affine(loaded, label):
-            g, b, m, v = (loaded[:, slot, 0:PACK] for slot in range(4))
+                nc.scalar.dma_start(out=loaded[:, slot, 0:PACK], in_=vec.rearrange("(q t) -> q t", t=PACK))
             spread = const.tile([P, PACK], F32, name=label + "_spread")
             gain = const.tile([P, PACK], F32, name=label + "_gain")
             offset = const.tile([P, PACK], F32, name=label + "_offset")
             shift = const.tile([P, PACK], F32, name=label + "_shift")
-            nc.vector.tensor_scalar_add(out=spread[:], in0=v, scalar1=BN_EPS)
+            nc.vector.tensor_scalar_add(out=spread[:], in0=loaded[:, 3, 0:PACK], scalar1=BN_EPS)
             nc.scalar.sqrt(out=spread[:], in_=spread[:])
             nc.vector.reciprocal(out=spread[:], in_=spread[:])
-            nc.vector.tensor_mul(out=gain[:], in0=g, in1=spread[:])
-            nc.vector.tensor_mul(out=offset[:], in0=gain[:], in1=m)
-            nc.vector.tensor_sub(out=shift[:], in0=b, in1=offset[:])
+            nc.vector.tensor_mul(out=gain[:], in0=loaded[:, 0, 0:PACK], in1=spread[:])
+            nc.vector.tensor_mul(out=offset[:], in0=gain[:], in1=loaded[:, 2, 0:PACK])
+            nc.vector.tensor_sub(out=shift[:], in0=loaded[:, 1, 0:PACK], in1=offset[:])
             return gain, shift
 
         def multiply(i):
@@ -121,39 +111,12 @@ def tile_p2b_xcorr_pb_kernel(tc, h2, W3, g3, b3, m3, v3, Wc1, gc1, bc1, mc1, vc1
                     start=True,
                     stop=True,
                 )
-                if i == PIECES - 1 and t >= PACK // 2:
-                    nc.vector.tensor_scalar(
-                        out=h3[i][:, t, :],
-                        in0=x3[:],
-                        scalar1=gain1[:, t : t + 1],
-                        scalar2=shift1[:, t : t + 1],
-                        op0=MULT,
-                        op1=ADD,
-                    )
-                else:
-                    nc.scalar.activation(
-                        out=h3[i][:, t, :], in_=x3[:], func=RELU, bias=shift1[:, t : t + 1], scale=gain1[:, t : t + 1]
-                    )
+                nc.scalar.activation(
+                    out=h3[i][:, t, :], in_=x3[:], func=RELU, bias=shift1[:, t : t + 1], scale=gain1[:, t : t + 1]
+                )
 
         def merge(i):
             nc.vector.tensor_max(out=best[:], in0=best[:], in1=h3[i][:])
-
-        def fold(x, label):
-            two = const.tile([P, PACK, 2 * N_SEARCH], BF16, name=label + "_two")
-            one = const.tile([P, PACK, N_SEARCH], BF16, name=label + "_one")
-            nc.vector.tensor_max(out=two[:], in0=x[:, :, : 2 * N_SEARCH], in1=x[:, :, 2 * N_SEARCH :])
-            nc.vector.tensor_max(out=one[:], in0=two[:, :, :N_SEARCH], in1=two[:, :, N_SEARCH:])
-            return one
-
-        load(0)
-        bn1_loaded = load_batch_norm(g3, b3, m3, v3, "bn1")
-        w3_sb = load_weight(W3, "w3")
-        load(1)
-        load(2)
-        wc_sb = load_weight(Wc1, "wc")
-        bn2_loaded = load_batch_norm(gc1, bc1, mc1, vc1, "bn2")
-        for i in range(3, RAW_BUFS):
-            load(i)
 
         warm = const.tile([P, 1], F32, name="warm")
         nc.vector.memset(warm[:], 1.0)
@@ -162,49 +125,57 @@ def tile_p2b_xcorr_pb_kernel(tc, h2, W3, g3, b3, m3, v3, Wc1, gc1, bc1, mc1, vc1
         make_identity(nc, identity[:])
         best = const.tile([P, PACK, COLS], BF16, name="best")
 
+        load(0)
+        gain1, shift1 = batch_norm_affine(g3, b3, m3, v3, "bn1")
         regroup(0)
         quantise(0)
-        gain1, shift1 = batch_norm_affine(bn1_loaded, "bn1")
-        w3_codes, w3_scales = quantise_weight(w3_sb, "w3")
+        w3_codes, w3_scales = prepare_weight(W3, "w3")
+        for i in range(1, RAW_BUFS):
+            load(i)
         regroup(1)
-        gain2, shift2 = batch_norm_affine(bn2_loaded, "bn2")
-        wc_codes, wc_scales = quantise_weight(wc_sb, "wc")
 
-        with tc.manual_schedule():
-            for i in range(PIECES):
-                if i + 1 < PIECES:
-                    quantise(i + 1)
-                if i + 2 < PIECES:
-                    regroup(i + 2)
-                multiply(i)
-                if i >= 2:
-                    merge(i - 1)
+        for i in range(PIECES):
+            multiply(i)
+            if i + 2 < PIECES:
+                regroup(i + 2)
+            if i + RAW_BUFS < PIECES:
+                load(i + RAW_BUFS)
+            if i + 1 < PIECES:
+                quantise(i + 1)
+            if i == 0:
+                wc_codes, wc_scales = prepare_weight(Wc1, "wc")
+                gain2, shift2 = batch_norm_affine(gc1, bc1, mc1, vc1, "bn2")
+            if i >= 2:
+                merge(i - 1)
+        merge(PIECES - 1)
 
-            earlier = fold(best, "earlier")
-            last = fold(h3[PIECES - 1], "last")
-            pooled = const.tile([P, N_SEARCH, PACK], BF16, name="pooled", align_bytes=64)
-            nc.vector.tensor_max(
-                out=pooled[:], in0=earlier[:].rearrange("p t n -> p n t"), in1=last[:].rearrange("p t n -> p n t")
+        half = const.tile([P, PACK, 2 * N_SEARCH], BF16, name="half")
+        nc.vector.tensor_max(out=half[:], in0=best[:, :, : 2 * N_SEARCH], in1=best[:, :, 2 * N_SEARCH :])
+        pooled = const.tile([P, N_SEARCH, PACK], BF16, name="pooled", align_bytes=64)
+        nc.vector.tensor_max(
+            out=pooled[:],
+            in0=half[:, :, :N_SEARCH].rearrange("p t n -> p n t"),
+            in1=half[:, :, N_SEARCH:].rearrange("p t n -> p n t"),
+        )
+        p_codes = const.tile([P, N_SEARCH], U32, name="p_codes", align_bytes=64)
+        p_scales = const.tile([P, N_SEARCH], U8, name="p_scales", align_bytes=64)
+        nc.vector.quantize_mx(
+            out=p_codes[:].bitcast(FP8X4), scales=p_scales[:], in_=pooled[:].rearrange("p n t -> p (n t)")
+        )
+        xc = side.tile([P, PACK, N_SEARCH], F32, name="xc", tag="side")
+        result = const.tile([P, PACK, N_SEARCH], F32, name="result")
+        for t in range(PACK):
+            nc.tensor.matmul_mx(
+                out=xc[:, t, :],
+                lhsT=wc_codes[:, t, :].bitcast(FP8X4),
+                lhsT_scale=wc_scales[:, t, :],
+                rhs=p_codes[:].bitcast(FP8X4),
+                rhs_scale=p_scales[:],
+                start=True,
+                stop=True,
             )
-            p_codes = const.tile([P, N_SEARCH], U32, name="p_codes", align_bytes=64)
-            p_scales = const.tile([P, N_SEARCH], U8, name="p_scales", align_bytes=64)
-            nc.vector.quantize_mx(
-                out=p_codes[:].bitcast(FP8X4), scales=p_scales[:], in_=pooled[:].rearrange("p n t -> p (n t)")
+        for t in range(PACK):
+            nc.scalar.activation(
+                out=result[:, t, :], in_=xc[:, t, :], func=RELU, bias=shift2[:, t : t + 1], scale=gain2[:, t : t + 1]
             )
-            xc = side.tile([P, PACK, N_SEARCH], F32, name="xc", tag="side")
-            result = const.tile([P, PACK, N_SEARCH], F32, name="result")
-            for t in range(PACK):
-                nc.tensor.matmul_mx(
-                    out=xc[:, t, :],
-                    lhsT=wc_codes[:, t, :].bitcast(FP8X4),
-                    lhsT_scale=wc_scales[:, t, :],
-                    rhs=p_codes[:].bitcast(FP8X4),
-                    rhs_scale=p_scales[:],
-                    start=True,
-                    stop=True,
-                )
-            for t in range(PACK):
-                nc.scalar.activation(
-                    out=result[:, t, :], in_=xc[:, t, :], func=RELU, bias=shift2[:, t : t + 1], scale=gain2[:, t : t + 1]
-                )
-            nc.sync.dma_start(out=out[0].rearrange("(q t) n -> q t n", t=PACK), in_=result[:])
+        nc.sync.dma_start(out=out[0].rearrange("(q t) n -> q t n", t=PACK), in_=result[:])

@@ -9,6 +9,7 @@ U32 = mybir.dt.uint32
 U8 = mybir.dt.uint8
 FP8X4 = mybir.dt.float8_e4m3fn_x4
 RELU = mybir.ActivationFunctionType.Relu
+ALU = mybir.AluOpType
 
 P = 128
 PACK = 4
@@ -18,8 +19,11 @@ N_SEARCH = 128
 COLS = 512
 PIECES = PAIRS // COLS
 RUN = 4
-SCALAR_COLS = 64
+GPSIMD_COLS = 240
 RAW_BUFS = 6
+GROUPED_BUFS = 3
+VECTOR_TILES = (0, 1)
+SCALAR_TILES = (2, 3)
 BN_EPS = 1e-5
 
 
@@ -30,30 +34,44 @@ def tile_p2b_xcorr_pb_kernel(tc, h2, W3, g3, b3, m3, v3, Wc1, gc1, bc1, mc1, vc1
     with (
         tc.tile_pool(name="const", bufs=1) as const,
         tc.tile_pool(name="raw", bufs=RAW_BUFS) as raw_pool,
-        tc.tile_pool(name="work", bufs=4) as work,
+        tc.tile_pool(name="regrouped", bufs=GROUPED_BUFS) as regrouped,
+        tc.tile_pool(name="work", bufs=3) as work,
         tc.tile_pool(name="packed", bufs=PIECES) as packed,
-        tc.psum_pool(name="banks", bufs=6) as banks,
-        tc.psum_pool(name="side", bufs=2) as side,
+        tc.psum_pool(name="banks", bufs=8) as banks,
     ):
         raw = {}
         grouped = {}
         codes = {}
         scales = {}
+        x3 = {}
         h3 = {}
 
         def load(i):
-            raw[i] = raw_pool.tile([P, PACK, COLS], BF16, name="raw")
-            nc.sync.dma_start(out=raw[i][:], in_=h2_rows[:, :, i * COLS : (i + 1) * COLS])
+            if i < PIECES:
+                raw[i] = raw_pool.tile([P, PACK, COLS], BF16, name="raw")
+                nc.sync.dma_start(out=raw[i][:], in_=h2_rows[:, :, i * COLS : (i + 1) * COLS])
 
         def regroup(i):
-            grouped[i] = work.tile([P, COLS, PACK], BF16, name="grouped", align_bytes=64)
+            if i >= PIECES:
+                return
+            grouped[i] = regrouped.tile([P, COLS, PACK], BF16, name="grouped", align_bytes=64)
+            nc.gpsimd.tensor_scalar(
+                out=grouped[i][:, :GPSIMD_COLS, :],
+                in0=raw[i][:, :, :GPSIMD_COLS].rearrange("p j w -> p w j"),
+                scalar1=1.0,
+                scalar2=0.0,
+                op0=ALU.mult,
+                op1=ALU.add,
+            )
             dst = grouped[i][:].rearrange("p (c r) j -> p c j r", r=RUN)
             src = raw[i][:].rearrange("p j (c r) -> p c j r", r=RUN)
-            cut = (COLS - SCALAR_COLS) // RUN
-            nc.vector.tensor_copy(out=dst[:, :cut], in_=src[:, :cut])
+            cut = GPSIMD_COLS // RUN
             nc.scalar.copy(out=dst[:, cut:], in_=src[:, cut:])
+            load(i + RAW_BUFS)
 
         def quantise(i):
+            if i >= PIECES:
+                return
             codes[i] = packed.tile([P, COLS], U32, name="codes", align_bytes=64)
             scales[i] = packed.tile([P, COLS], U8, name="scales", align_bytes=64)
             nc.vector.quantize_mx(
@@ -62,30 +80,38 @@ def tile_p2b_xcorr_pb_kernel(tc, h2, W3, g3, b3, m3, v3, Wc1, gc1, bc1, mc1, vc1
                 in_=grouped[i][:].rearrange("p w j -> p (w j)"),
             )
 
-        def prepare_weight(w, label):
+        def load_weight(w, label):
             w_sb = const.tile([P, PACK, H], BF16, name=label + "_sb")
             nc.sync.dma_start(out=w_sb[:], in_=w.rearrange("(q t) h -> q t h", t=PACK))
             w_codes = const.tile([P, PACK, P], U32, name=label + "_codes", align_bytes=64)
             w_scales = const.tile([P, PACK, P], U8, name=label + "_scales", align_bytes=64)
-            for t in range(PACK):
-                words = w_sb[:, t, :].bitcast(F32).rearrange("q (p u) -> q u p", u=2)
-                turned = side.tile([P, 2, P], F32, name="turned", tag="side")
-                for u in range(2):
-                    nc.tensor.transpose(turned[:, u, :], words[:, u, :], identity[:])
-                w_grouped = work.tile([P, H], BF16, name="w_grouped", align_bytes=64)
-                nc.scalar.copy(
-                    out=w_grouped[:].bitcast(F32).rearrange("p (q u) -> p q u", u=2),
-                    in_=turned[:].rearrange("p u q -> p q u"),
-                )
-                nc.vector.quantize_mx(
-                    out=w_codes[:, t, :].bitcast(FP8X4), scales=w_scales[:, t, :], in_=w_grouped[:]
-                )
-            return w_codes, w_scales
+            return w_sb, w_codes, w_scales
 
-        def batch_norm_affine(g, b, m, v, label):
+        def prepare_weight(weight, t, row_sign):
+            w_sb, w_codes, w_scales = weight
+            rows = w_sb[:, t, :]
+            if row_sign is not None:
+                signed = work.tile([P, H], BF16, name="signed")
+                nc.vector.tensor_scalar_mul(out=signed[:], in0=rows, scalar1=row_sign[:, t : t + 1])
+                rows = signed[:]
+            words = rows.bitcast(F32).rearrange("q (p u) -> q u p", u=2)
+            turned = banks.tile([P, 2, P], F32, name="turned", tag="x3")
+            for u in range(2):
+                nc.tensor.transpose(turned[:, u, :], words[:, u, :], identity[:])
+            w_grouped = work.tile([P, H], BF16, name="w_grouped", align_bytes=64)
+            nc.scalar.copy(
+                out=w_grouped[:].bitcast(F32).rearrange("p (q u) -> p q u", u=2),
+                in_=turned[:].rearrange("p u q -> p q u"),
+            )
+            nc.vector.quantize_mx(out=w_codes[:, t, :].bitcast(FP8X4), scales=w_scales[:, t, :], in_=w_grouped[:])
+
+        def load_batch_norm(g, b, m, v, label):
             loaded = const.tile([P, 4, 16], BF16, name=label + "_loaded")
             for slot, vec in enumerate((g, b, m, v)):
                 nc.scalar.dma_start(out=loaded[:, slot, 0:PACK], in_=vec.rearrange("(q t) -> q t", t=PACK))
+            return loaded
+
+        def batch_norm_affine(loaded, label):
             spread = const.tile([P, PACK], F32, name=label + "_spread")
             gain = const.tile([P, PACK], F32, name=label + "_gain")
             offset = const.tile([P, PACK], F32, name=label + "_offset")
@@ -99,76 +125,105 @@ def tile_p2b_xcorr_pb_kernel(tc, h2, W3, g3, b3, m3, v3, Wc1, gc1, bc1, mc1, vc1
             return gain, shift
 
         def multiply(i):
-            h3[i] = best if i == 0 else work.tile([P, PACK, COLS], BF16, name="h3")
             for t in range(PACK):
-                x3 = banks.tile([P, COLS], F32, name="x3")
+                x3[i, t] = banks.tile([P, COLS], F32, name="x3")
                 nc.tensor.matmul_mx(
-                    out=x3[:],
-                    lhsT=w3_codes[:, t, :].bitcast(FP8X4),
-                    lhsT_scale=w3_scales[:, t, :],
+                    out=x3[i, t][:],
+                    lhsT=w3[1][:, t, :].bitcast(FP8X4),
+                    lhsT_scale=w3[2][:, t, :],
                     rhs=codes[i][:].bitcast(FP8X4),
                     rhs_scale=scales[i][:],
                     start=True,
                     stop=True,
                 )
+
+        def pool_raw(i):
+            for s, t in enumerate(VECTOR_TILES):
+                if i == 0:
+                    nc.vector.tensor_copy(out=best_raw[:, s, :], in_=x3[i, t][:])
+                else:
+                    nc.vector.tensor_max(out=best_raw[:, s, :], in0=x3[i, t][:], in1=best_raw[:, s, :])
+
+        def activate(i):
+            h3[i] = best_act if i == 0 else work.tile([P, len(SCALAR_TILES), COLS], BF16, name="h3")
+            for s, t in enumerate(SCALAR_TILES):
                 nc.scalar.activation(
-                    out=h3[i][:, t, :], in_=x3[:], func=RELU, bias=shift1[:, t : t + 1], scale=gain1[:, t : t + 1]
+                    out=h3[i][:, s, :], in_=x3[i, t][:], func=RELU, bias=shift1[:, t : t + 1], scale=size1[:, t : t + 1]
                 )
 
         def merge(i):
-            nc.vector.tensor_max(out=best[:], in0=best[:], in1=h3[i][:])
+            if i >= 1:
+                nc.vector.tensor_max(out=best_act[:], in0=best_act[:], in1=h3[i][:])
 
         warm = const.tile([P, 1], F32, name="warm")
         nc.vector.memset(warm[:], 1.0)
         nc.scalar.sqrt(out=warm[:], in_=warm[:])
         identity = const.tile([P, P], F32, name="identity")
         make_identity(nc, identity[:])
-        best = const.tile([P, PACK, COLS], BF16, name="best")
+        best_raw = const.tile([P, len(VECTOR_TILES), COLS], F32, name="best_raw")
+        best_act = const.tile([P, len(SCALAR_TILES), COLS], BF16, name="best_act")
 
         load(0)
-        gain1, shift1 = batch_norm_affine(g3, b3, m3, v3, "bn1")
-        regroup(0)
-        quantise(0)
-        w3_codes, w3_scales = prepare_weight(W3, "w3")
+        gain1, shift1 = batch_norm_affine(load_batch_norm(g3, b3, m3, v3, "bn1"), "bn1")
+        w3 = load_weight(W3, "w3")
         for i in range(1, RAW_BUFS):
             load(i)
+        sign1 = const.tile([P, PACK], F32, name="sign1")
+        size1 = const.tile([P, PACK], F32, name="size1")
+        nc.vector.tensor_scalar(out=sign1[:], in0=gain1[:], scalar1=0.0, scalar2=2.0, op0=ALU.is_ge, op1=ALU.mult)
+        nc.vector.tensor_scalar_add(out=sign1[:], in0=sign1[:], scalar1=-1.0)
+        nc.vector.tensor_mul(out=size1[:], in0=gain1[:], in1=sign1[:])
+        regroup(0)
+        for t in range(PACK):
+            prepare_weight(w3, t, sign1)
+        quantise(0)
         regroup(1)
+        regroup(2)
+        wc = load_weight(Wc1, "wc")
+        bn2_loaded = load_batch_norm(gc1, bc1, mc1, vc1, "bn2")
 
-        for i in range(PIECES):
-            multiply(i)
-            if i + 2 < PIECES:
-                regroup(i + 2)
-            if i + RAW_BUFS < PIECES:
-                load(i + RAW_BUFS)
-            if i + 1 < PIECES:
+        with tc.manual_schedule():
+            for i in range(PIECES):
+                multiply(i)
                 quantise(i + 1)
-            if i == 0:
-                wc_codes, wc_scales = prepare_weight(Wc1, "wc")
-                gain2, shift2 = batch_norm_affine(gc1, bc1, mc1, vc1, "bn2")
-            if i >= 2:
+                pool_raw(i)
+                activate(i)
                 merge(i - 1)
+                regroup(i + GROUPED_BUFS)
+                if 4 <= i < 4 + PACK:
+                    prepare_weight(wc, i - 4, None)
+                if i == 4 + PACK:
+                    gain2, shift2 = batch_norm_affine(bn2_loaded, "bn2")
         merge(PIECES - 1)
 
-        half = const.tile([P, PACK, 2 * N_SEARCH], BF16, name="half")
-        nc.vector.tensor_max(out=half[:], in0=best[:, :, : 2 * N_SEARCH], in1=best[:, :, 2 * N_SEARCH :])
         pooled = const.tile([P, N_SEARCH, PACK], BF16, name="pooled", align_bytes=64)
+        half_raw = const.tile([P, len(VECTOR_TILES), 2 * N_SEARCH], F32, name="half_raw")
+        nc.vector.tensor_max(out=half_raw[:], in0=best_raw[:, :, : 2 * N_SEARCH], in1=best_raw[:, :, 2 * N_SEARCH :])
+        top_raw = const.tile([P, len(VECTOR_TILES), N_SEARCH], F32, name="top_raw")
+        nc.vector.tensor_max(out=top_raw[:], in0=half_raw[:, :, :N_SEARCH], in1=half_raw[:, :, N_SEARCH:])
+        for s, t in enumerate(VECTOR_TILES):
+            nc.scalar.activation(
+                out=pooled[:, :, t], in_=top_raw[:, s, :], func=RELU, bias=shift1[:, t : t + 1], scale=size1[:, t : t + 1]
+            )
+        half_act = const.tile([P, len(SCALAR_TILES), 2 * N_SEARCH], BF16, name="half_act")
+        nc.vector.tensor_max(out=half_act[:], in0=best_act[:, :, : 2 * N_SEARCH], in1=best_act[:, :, 2 * N_SEARCH :])
         nc.vector.tensor_max(
-            out=pooled[:],
-            in0=half[:, :, :N_SEARCH].rearrange("p t n -> p n t"),
-            in1=half[:, :, N_SEARCH:].rearrange("p t n -> p n t"),
+            out=pooled[:, :, SCALAR_TILES[0] : SCALAR_TILES[-1] + 1],
+            in0=half_act[:, :, :N_SEARCH].rearrange("p t n -> p n t"),
+            in1=half_act[:, :, N_SEARCH:].rearrange("p t n -> p n t"),
         )
         p_codes = const.tile([P, N_SEARCH], U32, name="p_codes", align_bytes=64)
         p_scales = const.tile([P, N_SEARCH], U8, name="p_scales", align_bytes=64)
         nc.vector.quantize_mx(
             out=p_codes[:].bitcast(FP8X4), scales=p_scales[:], in_=pooled[:].rearrange("p n t -> p (n t)")
         )
-        xc = side.tile([P, PACK, N_SEARCH], F32, name="xc", tag="side")
+        xc = banks.tile([P, PACK, N_SEARCH], F32, name="xc", tag="x3")
         result = const.tile([P, PACK, N_SEARCH], F32, name="result")
         for t in range(PACK):
             nc.tensor.matmul_mx(
                 out=xc[:, t, :],
-                lhsT=wc_codes[:, t, :].bitcast(FP8X4),
-                lhsT_scale=wc_scales[:, t, :],
+                lhsT=wc[1][:, t, :].bitcast(FP8X4),
+                lhsT_scale=wc[2][:, t, :],
                 rhs=p_codes[:].bitcast(FP8X4),
                 rhs_scale=p_scales[:],
                 start=True,

@@ -19,11 +19,15 @@ N_SEARCH = 128
 COLS = 512
 PIECES = PAIRS // COLS
 RUN = 4
-GPSIMD_COLS = 240
+GPSIMD_COLS = 128
+VECTOR_COLS = 96
+FIRST_VECTOR_COLS = 384
 RAW_BUFS = 6
 GROUPED_BUFS = 3
 VECTOR_TILES = (0, 1)
 SCALAR_TILES = (2, 3)
+TILE_ORDER = SCALAR_TILES + VECTOR_TILES
+WC_FROM = 4
 BN_EPS = 1e-5
 
 
@@ -35,9 +39,10 @@ def tile_p2b_xcorr_pb_kernel(tc, h2, W3, g3, b3, m3, v3, Wc1, gc1, bc1, mc1, vc1
         tc.tile_pool(name="const", bufs=1) as const,
         tc.tile_pool(name="raw", bufs=RAW_BUFS) as raw_pool,
         tc.tile_pool(name="regrouped", bufs=GROUPED_BUFS) as regrouped,
-        tc.tile_pool(name="work", bufs=3) as work,
+        tc.tile_pool(name="work", bufs=4) as work,
         tc.tile_pool(name="packed", bufs=PIECES) as packed,
         tc.psum_pool(name="banks", bufs=8) as banks,
+        tc.manual_schedule(),
     ):
         raw = {}
         grouped = {}
@@ -45,27 +50,31 @@ def tile_p2b_xcorr_pb_kernel(tc, h2, W3, g3, b3, m3, v3, Wc1, gc1, bc1, mc1, vc1
         scales = {}
         x3 = {}
         h3 = {}
+        w_grouped = {}
 
         def load(i):
             if i < PIECES:
                 raw[i] = raw_pool.tile([P, PACK, COLS], BF16, name="raw")
                 nc.sync.dma_start(out=raw[i][:], in_=h2_rows[:, :, i * COLS : (i + 1) * COLS])
 
-        def regroup(i):
+        def regroup(i, gpsimd_cols=GPSIMD_COLS, vector_cols=VECTOR_COLS):
             if i >= PIECES:
                 return
             grouped[i] = regrouped.tile([P, COLS, PACK], BF16, name="grouped", align_bytes=64)
-            nc.gpsimd.tensor_scalar(
-                out=grouped[i][:, :GPSIMD_COLS, :],
-                in0=raw[i][:, :, :GPSIMD_COLS].rearrange("p j w -> p w j"),
-                scalar1=1.0,
-                scalar2=0.0,
-                op0=ALU.mult,
-                op1=ALU.add,
-            )
+            if gpsimd_cols:
+                nc.gpsimd.tensor_scalar(
+                    out=grouped[i][:, :gpsimd_cols, :],
+                    in0=raw[i][:, :, :gpsimd_cols].rearrange("p j w -> p w j"),
+                    scalar1=1.0,
+                    scalar2=0.0,
+                    op0=ALU.mult,
+                    op1=ALU.add,
+                )
             dst = grouped[i][:].rearrange("p (c r) j -> p c j r", r=RUN)
             src = raw[i][:].rearrange("p j (c r) -> p c j r", r=RUN)
-            cut = GPSIMD_COLS // RUN
+            first = gpsimd_cols // RUN
+            cut = (gpsimd_cols + vector_cols) // RUN
+            nc.vector.tensor_copy(out=dst[:, first:cut], in_=src[:, first:cut])
             nc.scalar.copy(out=dst[:, cut:], in_=src[:, cut:])
             load(i + RAW_BUFS)
 
@@ -87,9 +96,8 @@ def tile_p2b_xcorr_pb_kernel(tc, h2, W3, g3, b3, m3, v3, Wc1, gc1, bc1, mc1, vc1
             w_scales = const.tile([P, PACK, P], U8, name=label + "_scales", align_bytes=64)
             return w_sb, w_codes, w_scales
 
-        def prepare_weight(weight, t, row_sign):
-            w_sb, w_codes, w_scales = weight
-            rows = w_sb[:, t, :]
+        def turn_weight(weight, t, row_sign):
+            rows = weight[0][:, t, :]
             if row_sign is not None:
                 signed = work.tile([P, H], BF16, name="signed")
                 nc.vector.tensor_scalar_mul(out=signed[:], in0=rows, scalar1=row_sign[:, t : t + 1])
@@ -98,34 +106,19 @@ def tile_p2b_xcorr_pb_kernel(tc, h2, W3, g3, b3, m3, v3, Wc1, gc1, bc1, mc1, vc1
             turned = banks.tile([P, 2, P], F32, name="turned", tag="x3")
             for u in range(2):
                 nc.tensor.transpose(turned[:, u, :], words[:, u, :], identity[:])
-            w_grouped = work.tile([P, H], BF16, name="w_grouped", align_bytes=64)
+            w_grouped[t] = work.tile([P, H], BF16, name="w_grouped", align_bytes=64)
             nc.scalar.copy(
-                out=w_grouped[:].bitcast(F32).rearrange("p (q u) -> p q u", u=2),
+                out=w_grouped[t][:].bitcast(F32).rearrange("p (q u) -> p q u", u=2),
                 in_=turned[:].rearrange("p u q -> p q u"),
             )
-            nc.vector.quantize_mx(out=w_codes[:, t, :].bitcast(FP8X4), scales=w_scales[:, t, :], in_=w_grouped[:])
 
-        def load_batch_norm(g, b, m, v, label):
-            loaded = const.tile([P, 4, 16], BF16, name=label + "_loaded")
-            for slot, vec in enumerate((g, b, m, v)):
-                nc.scalar.dma_start(out=loaded[:, slot, 0:PACK], in_=vec.rearrange("(q t) -> q t", t=PACK))
-            return loaded
-
-        def batch_norm_affine(loaded, label):
-            spread = const.tile([P, PACK], F32, name=label + "_spread")
-            gain = const.tile([P, PACK], F32, name=label + "_gain")
-            offset = const.tile([P, PACK], F32, name=label + "_offset")
-            shift = const.tile([P, PACK], F32, name=label + "_shift")
-            nc.vector.tensor_scalar_add(out=spread[:], in0=loaded[:, 3, 0:PACK], scalar1=BN_EPS)
-            nc.scalar.sqrt(out=spread[:], in_=spread[:])
-            nc.vector.reciprocal(out=spread[:], in_=spread[:])
-            nc.vector.tensor_mul(out=gain[:], in0=loaded[:, 0, 0:PACK], in1=spread[:])
-            nc.vector.tensor_mul(out=offset[:], in0=gain[:], in1=loaded[:, 2, 0:PACK])
-            nc.vector.tensor_sub(out=shift[:], in0=loaded[:, 1, 0:PACK], in1=offset[:])
-            return gain, shift
+        def pack_weight(weight, t):
+            nc.vector.quantize_mx(
+                out=weight[1][:, t, :].bitcast(FP8X4), scales=weight[2][:, t, :], in_=w_grouped[t][:]
+            )
 
         def multiply(i):
-            for t in range(PACK):
+            for t in TILE_ORDER:
                 x3[i, t] = banks.tile([P, COLS], F32, name="x3")
                 nc.tensor.matmul_mx(
                     out=x3[i, t][:],
@@ -148,12 +141,26 @@ def tile_p2b_xcorr_pb_kernel(tc, h2, W3, g3, b3, m3, v3, Wc1, gc1, bc1, mc1, vc1
             h3[i] = best_act if i == 0 else work.tile([P, len(SCALAR_TILES), COLS], BF16, name="h3")
             for s, t in enumerate(SCALAR_TILES):
                 nc.scalar.activation(
-                    out=h3[i][:, s, :], in_=x3[i, t][:], func=RELU, bias=shift1[:, t : t + 1], scale=size1[:, t : t + 1]
+                    out=h3[i][:, s, :],
+                    in_=x3[i, t][:],
+                    func=RELU,
+                    bias=shift[:, 0, t : t + 1],
+                    scale=gain[:, 0, t : t + 1],
                 )
 
         def merge(i):
             if i >= 1:
                 nc.vector.tensor_max(out=best_act[:], in0=best_act[:], in1=h3[i][:])
+
+        bn_loaded = const.tile([P, 2, 4, 16], BF16, name="bn_loaded")
+        for layer, vectors in enumerate(((g3, b3, m3, v3), (gc1, bc1, mc1, vc1))):
+            for slot, vec in enumerate(vectors):
+                nc.scalar.dma_start(out=bn_loaded[:, layer, slot, 0:PACK], in_=vec.rearrange("(q t) -> q t", t=PACK))
+        load(0)
+        w3 = load_weight(W3, "w3")
+        for i in range(1, RAW_BUFS):
+            load(i)
+        wc = load_weight(Wc1, "wc")
 
         warm = const.tile([P, 1], F32, name="warm")
         nc.vector.memset(warm[:], 1.0)
@@ -163,38 +170,44 @@ def tile_p2b_xcorr_pb_kernel(tc, h2, W3, g3, b3, m3, v3, Wc1, gc1, bc1, mc1, vc1
         best_raw = const.tile([P, len(VECTOR_TILES), COLS], F32, name="best_raw")
         best_act = const.tile([P, len(SCALAR_TILES), COLS], BF16, name="best_act")
 
-        load(0)
-        gain1, shift1 = batch_norm_affine(load_batch_norm(g3, b3, m3, v3, "bn1"), "bn1")
-        w3 = load_weight(W3, "w3")
-        for i in range(1, RAW_BUFS):
-            load(i)
+        spread = const.tile([P, 2, PACK], F32, name="spread")
+        gain = const.tile([P, 2, PACK], F32, name="gain")
+        offset = const.tile([P, 2, PACK], F32, name="offset")
+        shift = const.tile([P, 2, PACK], F32, name="shift")
         sign1 = const.tile([P, PACK], F32, name="sign1")
         size1 = const.tile([P, PACK], F32, name="size1")
-        nc.vector.tensor_scalar(out=sign1[:], in0=gain1[:], scalar1=0.0, scalar2=2.0, op0=ALU.is_ge, op1=ALU.mult)
+        nc.vector.tensor_scalar_add(out=spread[:], in0=bn_loaded[:, :, 3, 0:PACK], scalar1=BN_EPS)
+        nc.scalar.sqrt(out=spread[:], in_=spread[:])
+        nc.vector.tensor_scalar(
+            out=sign1[:], in0=bn_loaded[:, 0, 0, 0:PACK], scalar1=0.0, scalar2=2.0, op0=ALU.is_ge, op1=ALU.mult
+        )
         nc.vector.tensor_scalar_add(out=sign1[:], in0=sign1[:], scalar1=-1.0)
-        nc.vector.tensor_mul(out=size1[:], in0=gain1[:], in1=sign1[:])
-        regroup(0)
-        for t in range(PACK):
-            prepare_weight(w3, t, sign1)
+
+        regroup(0, 0, FIRST_VECTOR_COLS)
+        for t in TILE_ORDER:
+            turn_weight(w3, t, sign1 if t in VECTOR_TILES else None)
         quantise(0)
+        nc.vector.reciprocal(out=spread[:], in_=spread[:])
+        nc.vector.tensor_mul(out=gain[:], in0=bn_loaded[:, :, 0, 0:PACK], in1=spread[:])
+        nc.vector.tensor_mul(out=offset[:], in0=gain[:], in1=bn_loaded[:, :, 2, 0:PACK])
+        nc.vector.tensor_sub(out=shift[:], in0=bn_loaded[:, :, 1, 0:PACK], in1=offset[:])
+        nc.vector.tensor_mul(out=size1[:], in0=gain[:, 0, :], in1=sign1[:])
+        for t in TILE_ORDER:
+            pack_weight(w3, t)
         regroup(1)
         regroup(2)
-        wc = load_weight(Wc1, "wc")
-        bn2_loaded = load_batch_norm(gc1, bc1, mc1, vc1, "bn2")
 
-        with tc.manual_schedule():
-            for i in range(PIECES):
-                multiply(i)
-                quantise(i + 1)
-                pool_raw(i)
-                activate(i)
-                merge(i - 1)
-                regroup(i + GROUPED_BUFS)
-                if 4 <= i < 4 + PACK:
-                    prepare_weight(wc, i - 4, None)
-                if i == 4 + PACK:
-                    gain2, shift2 = batch_norm_affine(bn2_loaded, "bn2")
-        merge(PIECES - 1)
+        for i in range(PIECES):
+            multiply(i)
+            quantise(i + 1)
+            pool_raw(i)
+            activate(i)
+            merge(i - 1)
+            regroup(i + GROUPED_BUFS)
+            if WC_FROM < i <= WC_FROM + PACK:
+                pack_weight(wc, i - WC_FROM - 1)
+            if WC_FROM <= i < WC_FROM + PACK:
+                turn_weight(wc, i - WC_FROM, None)
 
         pooled = const.tile([P, N_SEARCH, PACK], BF16, name="pooled", align_bytes=64)
         half_raw = const.tile([P, len(VECTOR_TILES), 2 * N_SEARCH], F32, name="half_raw")
@@ -203,8 +216,9 @@ def tile_p2b_xcorr_pb_kernel(tc, h2, W3, g3, b3, m3, v3, Wc1, gc1, bc1, mc1, vc1
         nc.vector.tensor_max(out=top_raw[:], in0=half_raw[:, :, :N_SEARCH], in1=half_raw[:, :, N_SEARCH:])
         for s, t in enumerate(VECTOR_TILES):
             nc.scalar.activation(
-                out=pooled[:, :, t], in_=top_raw[:, s, :], func=RELU, bias=shift1[:, t : t + 1], scale=size1[:, t : t + 1]
+                out=pooled[:, :, t], in_=top_raw[:, s, :], func=RELU, bias=shift[:, 0, t : t + 1], scale=size1[:, t : t + 1]
             )
+        merge(PIECES - 1)
         half_act = const.tile([P, len(SCALAR_TILES), 2 * N_SEARCH], BF16, name="half_act")
         nc.vector.tensor_max(out=half_act[:], in0=best_act[:, :, : 2 * N_SEARCH], in1=best_act[:, :, 2 * N_SEARCH :])
         nc.vector.tensor_max(
@@ -231,6 +245,6 @@ def tile_p2b_xcorr_pb_kernel(tc, h2, W3, g3, b3, m3, v3, Wc1, gc1, bc1, mc1, vc1
             )
         for t in range(PACK):
             nc.scalar.activation(
-                out=result[:, t, :], in_=xc[:, t, :], func=RELU, bias=shift2[:, t : t + 1], scale=gain2[:, t : t + 1]
+                out=result[:, t, :], in_=xc[:, t, :], func=RELU, bias=shift[:, 1, t : t + 1], scale=gain[:, 1, t : t + 1]
             )
         nc.sync.dma_start(out=out[0].rearrange("(q t) n -> q t n", t=PACK), in_=result[:])

@@ -22,12 +22,14 @@ RUN = 4
 GPSIMD_COLS = 128
 VECTOR_COLS = 96
 FIRST_VECTOR_COLS = 384
+EARLY_VECTOR_COLS = 224
 RAW_BUFS = 6
 GROUPED_BUFS = 3
 VECTOR_TILES = (0, 1)
 SCALAR_TILES = (2, 3)
 TILE_ORDER = SCALAR_TILES + VECTOR_TILES
 WC_FROM = 4
+BN2_AT = 10
 BN_EPS = 1e-5
 
 
@@ -144,23 +146,43 @@ def tile_p2b_xcorr_pb_kernel(tc, h2, W3, g3, b3, m3, v3, Wc1, gc1, bc1, mc1, vc1
                     out=h3[i][:, s, :],
                     in_=x3[i, t][:],
                     func=RELU,
-                    bias=shift[:, 0, t : t + 1],
-                    scale=gain[:, 0, t : t + 1],
+                    bias=shift1[:, t : t + 1],
+                    scale=gain1[:, t : t + 1],
                 )
 
         def merge(i):
             if i >= 1:
                 nc.vector.tensor_max(out=best_act[:], in0=best_act[:], in1=h3[i][:])
 
-        bn_loaded = const.tile([P, 2, 4, 16], BF16, name="bn_loaded")
-        for layer, vectors in enumerate(((g3, b3, m3, v3), (gc1, bc1, mc1, vc1))):
-            for slot, vec in enumerate(vectors):
-                nc.scalar.dma_start(out=bn_loaded[:, layer, slot, 0:PACK], in_=vec.rearrange("(q t) -> q t", t=PACK))
+        def load_batch_norm(queue, g, b, m, v, label):
+            loaded = const.tile([P, 4, 16], BF16, name=label + "_loaded")
+            for slot, vec in enumerate((g, b, m, v)):
+                queue.dma_start(out=loaded[:, slot, 0:PACK], in_=vec.rearrange("(q t) -> q t", t=PACK))
+            return loaded
+
+        def start_batch_norm(loaded, label):
+            spread = const.tile([P, PACK], F32, name=label + "_spread")
+            nc.vector.tensor_scalar_add(out=spread[:], in0=loaded[:, 3, 0:PACK], scalar1=BN_EPS)
+            nc.scalar.sqrt(out=spread[:], in_=spread[:])
+            return spread
+
+        def finish_batch_norm(loaded, spread, label):
+            gain = const.tile([P, PACK], F32, name=label + "_gain")
+            offset = const.tile([P, PACK], F32, name=label + "_offset")
+            shift = const.tile([P, PACK], F32, name=label + "_shift")
+            nc.vector.reciprocal(out=spread[:], in_=spread[:])
+            nc.vector.tensor_mul(out=gain[:], in0=loaded[:, 0, 0:PACK], in1=spread[:])
+            nc.vector.tensor_mul(out=offset[:], in0=gain[:], in1=loaded[:, 2, 0:PACK])
+            nc.vector.tensor_sub(out=shift[:], in0=loaded[:, 1, 0:PACK], in1=offset[:])
+            return gain, shift
+
+        bn1_loaded = load_batch_norm(nc.sync, g3, b3, m3, v3, "bn1")
         load(0)
         w3 = load_weight(W3, "w3")
         for i in range(1, RAW_BUFS):
             load(i)
         wc = load_weight(Wc1, "wc")
+        bn2_loaded = load_batch_norm(nc.sync, gc1, bc1, mc1, vc1, "bn2")
 
         warm = const.tile([P, 1], F32, name="warm")
         nc.vector.memset(warm[:], 1.0)
@@ -170,32 +192,24 @@ def tile_p2b_xcorr_pb_kernel(tc, h2, W3, g3, b3, m3, v3, Wc1, gc1, bc1, mc1, vc1
         best_raw = const.tile([P, len(VECTOR_TILES), COLS], F32, name="best_raw")
         best_act = const.tile([P, len(SCALAR_TILES), COLS], BF16, name="best_act")
 
-        spread = const.tile([P, 2, PACK], F32, name="spread")
-        gain = const.tile([P, 2, PACK], F32, name="gain")
-        offset = const.tile([P, 2, PACK], F32, name="offset")
-        shift = const.tile([P, 2, PACK], F32, name="shift")
+        spread1 = start_batch_norm(bn1_loaded, "bn1")
         sign1 = const.tile([P, PACK], F32, name="sign1")
         size1 = const.tile([P, PACK], F32, name="size1")
-        nc.vector.tensor_scalar_add(out=spread[:], in0=bn_loaded[:, :, 3, 0:PACK], scalar1=BN_EPS)
-        nc.scalar.sqrt(out=spread[:], in_=spread[:])
         nc.vector.tensor_scalar(
-            out=sign1[:], in0=bn_loaded[:, 0, 0, 0:PACK], scalar1=0.0, scalar2=2.0, op0=ALU.is_ge, op1=ALU.mult
+            out=sign1[:], in0=bn1_loaded[:, 0, 0:PACK], scalar1=0.0, scalar2=2.0, op0=ALU.is_ge, op1=ALU.mult
         )
         nc.vector.tensor_scalar_add(out=sign1[:], in0=sign1[:], scalar1=-1.0)
+        gain1, shift1 = finish_batch_norm(bn1_loaded, spread1, "bn1")
+        nc.vector.tensor_mul(out=size1[:], in0=gain1[:], in1=sign1[:])
 
         regroup(0, 0, FIRST_VECTOR_COLS)
         for t in TILE_ORDER:
             turn_weight(w3, t, sign1 if t in VECTOR_TILES else None)
         quantise(0)
-        nc.vector.reciprocal(out=spread[:], in_=spread[:])
-        nc.vector.tensor_mul(out=gain[:], in0=bn_loaded[:, :, 0, 0:PACK], in1=spread[:])
-        nc.vector.tensor_mul(out=offset[:], in0=gain[:], in1=bn_loaded[:, :, 2, 0:PACK])
-        nc.vector.tensor_sub(out=shift[:], in0=bn_loaded[:, :, 1, 0:PACK], in1=offset[:])
-        nc.vector.tensor_mul(out=size1[:], in0=gain[:, 0, :], in1=sign1[:])
         for t in TILE_ORDER:
             pack_weight(w3, t)
-        regroup(1)
-        regroup(2)
+        for i in range(1, GROUPED_BUFS):
+            regroup(i, GPSIMD_COLS, EARLY_VECTOR_COLS)
 
         for i in range(PIECES):
             multiply(i)
@@ -208,6 +222,10 @@ def tile_p2b_xcorr_pb_kernel(tc, h2, W3, g3, b3, m3, v3, Wc1, gc1, bc1, mc1, vc1
                 pack_weight(wc, i - WC_FROM - 1)
             if WC_FROM <= i < WC_FROM + PACK:
                 turn_weight(wc, i - WC_FROM, None)
+            if i == BN2_AT:
+                spread2 = start_batch_norm(bn2_loaded, "bn2")
+            if i == BN2_AT + 1:
+                gain2, shift2 = finish_batch_norm(bn2_loaded, spread2, "bn2")
 
         pooled = const.tile([P, N_SEARCH, PACK], BF16, name="pooled", align_bytes=64)
         half_raw = const.tile([P, len(VECTOR_TILES), 2 * N_SEARCH], F32, name="half_raw")
@@ -216,7 +234,7 @@ def tile_p2b_xcorr_pb_kernel(tc, h2, W3, g3, b3, m3, v3, Wc1, gc1, bc1, mc1, vc1
         nc.vector.tensor_max(out=top_raw[:], in0=half_raw[:, :, :N_SEARCH], in1=half_raw[:, :, N_SEARCH:])
         for s, t in enumerate(VECTOR_TILES):
             nc.scalar.activation(
-                out=pooled[:, :, t], in_=top_raw[:, s, :], func=RELU, bias=shift[:, 0, t : t + 1], scale=size1[:, t : t + 1]
+                out=pooled[:, :, t], in_=top_raw[:, s, :], func=RELU, bias=shift1[:, t : t + 1], scale=size1[:, t : t + 1]
             )
         merge(PIECES - 1)
         half_act = const.tile([P, len(SCALAR_TILES), 2 * N_SEARCH], BF16, name="half_act")
@@ -245,6 +263,6 @@ def tile_p2b_xcorr_pb_kernel(tc, h2, W3, g3, b3, m3, v3, Wc1, gc1, bc1, mc1, vc1
             )
         for t in range(PACK):
             nc.scalar.activation(
-                out=result[:, t, :], in_=xc[:, t, :], func=RELU, bias=shift[:, 1, t : t + 1], scale=gain[:, 1, t : t + 1]
+                out=result[:, t, :], in_=xc[:, t, :], func=RELU, bias=shift2[:, t : t + 1], scale=gain2[:, t : t + 1]
             )
         nc.sync.dma_start(out=out[0].rearrange("(q t) n -> q t n", t=PACK), in_=result[:])

@@ -20,9 +20,10 @@ COLS = 512
 PIECES = PAIRS // COLS
 RUN = 4
 GPSIMD_COLS = 128
-VECTOR_COLS = 96
-FIRST_VECTOR_COLS = 384
-EARLY_VECTOR_COLS = 224
+TENSOR_COLS = 192
+VECTOR_COLS = 32
+FIRST_VECTOR_COLS = 256
+EARLY_VECTOR_COLS = 128
 RAW_BUFS = 6
 GROUPED_BUFS = 3
 VECTOR_TILES = (0, 1)
@@ -43,7 +44,8 @@ def tile_p2b_xcorr_pb_kernel(tc, h2, W3, g3, b3, m3, v3, Wc1, gc1, bc1, mc1, vc1
         tc.tile_pool(name="regrouped", bufs=GROUPED_BUFS) as regrouped,
         tc.tile_pool(name="work", bufs=4) as work,
         tc.tile_pool(name="packed", bufs=PIECES) as packed,
-        tc.psum_pool(name="banks", bufs=8) as banks,
+        tc.psum_pool(name="banks", bufs=6) as banks,
+        tc.psum_pool(name="passing", bufs=2) as passing,
         tc.manual_schedule(),
     ):
         raw = {}
@@ -72,10 +74,21 @@ def tile_p2b_xcorr_pb_kernel(tc, h2, W3, g3, b3, m3, v3, Wc1, gc1, bc1, mc1, vc1
                     op0=ALU.mult,
                     op1=ALU.add,
                 )
+            passed_to = gpsimd_cols + TENSOR_COLS
+            passed = passing.tile([P, TENSOR_COLS, PACK], BF16, name="passed")
+            for u in range(PACK // 2):
+                nc.tensor.matmul(
+                    out=passed[:, :, 2 * u : 2 * u + 2],
+                    lhsT=identity_bf[:],
+                    rhs=raw[i][:, 2 * u : 2 * u + 2, gpsimd_cols:passed_to].rearrange("p j w -> p w j"),
+                    start=True,
+                    stop=True,
+                )
+            nc.scalar.copy(out=grouped[i][:, gpsimd_cols:passed_to, :], in_=passed[:])
             dst = grouped[i][:].rearrange("p (c r) j -> p c j r", r=RUN)
             src = raw[i][:].rearrange("p j (c r) -> p c j r", r=RUN)
-            first = gpsimd_cols // RUN
-            cut = (gpsimd_cols + vector_cols) // RUN
+            first = passed_to // RUN
+            cut = (passed_to + vector_cols) // RUN
             nc.vector.tensor_copy(out=dst[:, first:cut], in_=src[:, first:cut])
             nc.scalar.copy(out=dst[:, cut:], in_=src[:, cut:])
             load(i + RAW_BUFS)
@@ -189,6 +202,8 @@ def tile_p2b_xcorr_pb_kernel(tc, h2, W3, g3, b3, m3, v3, Wc1, gc1, bc1, mc1, vc1
         nc.scalar.sqrt(out=warm[:], in_=warm[:])
         identity = const.tile([P, P], F32, name="identity")
         make_identity(nc, identity[:])
+        identity_bf = const.tile([P, P], BF16, name="identity_bf")
+        make_identity(nc, identity_bf[:])
         best_raw = const.tile([P, len(VECTOR_TILES), COLS], F32, name="best_raw")
         best_act = const.tile([P, len(SCALAR_TILES), COLS], BF16, name="best_act")
 

@@ -19,11 +19,11 @@ N_SEARCH = 128
 COLS = 512
 PIECES = PAIRS // COLS
 RUN = 4
-GPSIMD_COLS = 128
+GPSIMD_COLS = 176
 TENSOR_COLS = 192
-VECTOR_COLS = 32
+VECTOR_COLS = 0
 FIRST_VECTOR_COLS = 256
-EARLY_VECTOR_COLS = 128
+EARLY_VECTOR_COLS = 192
 RAW_BUFS = 6
 GROUPED_BUFS = 3
 VECTOR_TILES = (0, 1)
@@ -89,7 +89,8 @@ def tile_p2b_xcorr_pb_kernel(tc, h2, W3, g3, b3, m3, v3, Wc1, gc1, bc1, mc1, vc1
             src = raw[i][:].rearrange("p j (c r) -> p c j r", r=RUN)
             first = passed_to // RUN
             cut = (passed_to + vector_cols) // RUN
-            nc.vector.tensor_copy(out=dst[:, first:cut], in_=src[:, first:cut])
+            if vector_cols:
+                nc.vector.tensor_copy(out=dst[:, first:cut], in_=src[:, first:cut])
             nc.scalar.copy(out=dst[:, cut:], in_=src[:, cut:])
             load(i + RAW_BUFS)
 
@@ -224,14 +225,14 @@ def tile_p2b_xcorr_pb_kernel(tc, h2, W3, g3, b3, m3, v3, Wc1, gc1, bc1, mc1, vc1
         for t in TILE_ORDER:
             pack_weight(w3, t)
         for i in range(1, GROUPED_BUFS):
-            regroup(i, GPSIMD_COLS, EARLY_VECTOR_COLS)
+            regroup(i, 0, EARLY_VECTOR_COLS)
 
         for i in range(PIECES):
             multiply(i)
             quantise(i + 1)
+            merge(i - 1)
             pool_raw(i)
             activate(i)
-            merge(i - 1)
             regroup(i + GROUPED_BUFS)
             if WC_FROM < i <= WC_FROM + PACK:
                 pack_weight(wc, i - WC_FROM - 1)

@@ -19,19 +19,26 @@ N_SEARCH = 128
 COLS = 512
 PIECES = PAIRS // COLS
 RUN = 4
-GPSIMD_COLS = 176
-TENSOR_COLS = 192
-VECTOR_COLS = 0
+GPSIMD_COLS = 192
+TENSOR_COLS = 204
 FIRST_VECTOR_COLS = 256
-EARLY_VECTOR_COLS = 192
 RAW_BUFS = 6
-GROUPED_BUFS = 3
+AHEAD = 3
+MERGE_LAG = 2
 VECTOR_TILES = (0, 1)
 SCALAR_TILES = (2, 3)
 TILE_ORDER = SCALAR_TILES + VECTOR_TILES
 WC_FROM = 4
 BN2_AT = 10
 BN_EPS = 1e-5
+
+
+def shares(i):
+    if i == 0:
+        return 0, FIRST_VECTOR_COLS
+    if i <= AHEAD:
+        return 0, GPSIMD_COLS
+    return GPSIMD_COLS, 0
 
 
 def tile_p2b_xcorr_pb_kernel(tc, h2, W3, g3, b3, m3, v3, Wc1, gc1, bc1, mc1, vc1, out):
@@ -41,7 +48,7 @@ def tile_p2b_xcorr_pb_kernel(tc, h2, W3, g3, b3, m3, v3, Wc1, gc1, bc1, mc1, vc1
     with (
         tc.tile_pool(name="const", bufs=1) as const,
         tc.tile_pool(name="raw", bufs=RAW_BUFS) as raw_pool,
-        tc.tile_pool(name="regrouped", bufs=GROUPED_BUFS) as regrouped,
+        tc.tile_pool(name="regrouped", bufs=AHEAD) as regrouped,
         tc.tile_pool(name="work", bufs=4) as work,
         tc.tile_pool(name="packed", bufs=PIECES) as packed,
         tc.psum_pool(name="banks", bufs=6) as banks,
@@ -50,6 +57,7 @@ def tile_p2b_xcorr_pb_kernel(tc, h2, W3, g3, b3, m3, v3, Wc1, gc1, bc1, mc1, vc1
     ):
         raw = {}
         grouped = {}
+        passed = {}
         codes = {}
         scales = {}
         x3 = {}
@@ -61,9 +69,10 @@ def tile_p2b_xcorr_pb_kernel(tc, h2, W3, g3, b3, m3, v3, Wc1, gc1, bc1, mc1, vc1
                 raw[i] = raw_pool.tile([P, PACK, COLS], BF16, name="raw")
                 nc.sync.dma_start(out=raw[i][:], in_=h2_rows[:, :, i * COLS : (i + 1) * COLS])
 
-        def regroup(i, gpsimd_cols=GPSIMD_COLS, vector_cols=VECTOR_COLS):
+        def start_regroup(i):
             if i >= PIECES:
                 return
+            gpsimd_cols = shares(i)[0]
             grouped[i] = regrouped.tile([P, COLS, PACK], BF16, name="grouped", align_bytes=64)
             if gpsimd_cols:
                 nc.gpsimd.tensor_scalar(
@@ -74,23 +83,33 @@ def tile_p2b_xcorr_pb_kernel(tc, h2, W3, g3, b3, m3, v3, Wc1, gc1, bc1, mc1, vc1
                     op0=ALU.mult,
                     op1=ALU.add,
                 )
-            passed_to = gpsimd_cols + TENSOR_COLS
-            passed = passing.tile([P, TENSOR_COLS, PACK], BF16, name="passed")
+            passed[i] = passing.tile([P, TENSOR_COLS, PACK], BF16, name="passed")
             for u in range(PACK // 2):
                 nc.tensor.matmul(
-                    out=passed[:, :, 2 * u : 2 * u + 2],
+                    out=passed[i][:, :, 2 * u : 2 * u + 2],
                     lhsT=identity_bf[:],
-                    rhs=raw[i][:, 2 * u : 2 * u + 2, gpsimd_cols:passed_to].rearrange("p j w -> p w j"),
+                    rhs=raw[i][:, 2 * u : 2 * u + 2, gpsimd_cols : gpsimd_cols + TENSOR_COLS].rearrange("p j w -> p w j"),
                     start=True,
                     stop=True,
                 )
-            nc.scalar.copy(out=grouped[i][:, gpsimd_cols:passed_to, :], in_=passed[:])
+
+        def runs(i):
             dst = grouped[i][:].rearrange("p (c r) j -> p c j r", r=RUN)
             src = raw[i][:].rearrange("p j (c r) -> p c j r", r=RUN)
-            first = passed_to // RUN
-            cut = (passed_to + vector_cols) // RUN
-            if vector_cols:
+            first = (shares(i)[0] + TENSOR_COLS) // RUN
+            return dst, src, first, first + shares(i)[1] // RUN
+
+        def vector_regroup(i):
+            if i < PIECES and shares(i)[1]:
+                dst, src, first, cut = runs(i)
                 nc.vector.tensor_copy(out=dst[:, first:cut], in_=src[:, first:cut])
+
+        def scalar_regroup(i):
+            if i >= PIECES:
+                return
+            gpsimd_cols = shares(i)[0]
+            nc.scalar.copy(out=grouped[i][:, gpsimd_cols : gpsimd_cols + TENSOR_COLS, :], in_=passed[i][:])
+            dst, src, first, cut = runs(i)
             nc.scalar.copy(out=dst[:, cut:], in_=src[:, cut:])
             load(i + RAW_BUFS)
 
@@ -147,26 +166,31 @@ def tile_p2b_xcorr_pb_kernel(tc, h2, W3, g3, b3, m3, v3, Wc1, gc1, bc1, mc1, vc1
                 )
 
         def pool_raw(i):
-            for s, t in enumerate(VECTOR_TILES):
+            for t in VECTOR_TILES:
                 if i == 0:
-                    nc.vector.tensor_copy(out=best_raw[:, s, :], in_=x3[i, t][:])
+                    nc.vector.tensor_copy(out=best_raw[:, t, :], in_=x3[i, t][:])
                 else:
-                    nc.vector.tensor_max(out=best_raw[:, s, :], in0=x3[i, t][:], in1=best_raw[:, s, :])
+                    nc.vector.tensor_max(out=best_raw[:, t, :], in0=x3[i, t][:], in1=best_raw[:, t, :])
+
+        def norm_relu(dst, src, t):
+            nc.scalar.activation(
+                out=dst,
+                in_=src,
+                func=RELU,
+                bias=shift1[:, t : t + 1],
+                scale=(size1 if t in VECTOR_TILES else gain1)[:, t : t + 1],
+            )
 
         def activate(i):
-            h3[i] = best_act if i == 0 else work.tile([P, len(SCALAR_TILES), COLS], BF16, name="h3")
+            if i > 0:
+                h3[i] = work.tile([P, len(SCALAR_TILES), COLS], BF16, name="h3")
             for s, t in enumerate(SCALAR_TILES):
-                nc.scalar.activation(
-                    out=h3[i][:, s, :],
-                    in_=x3[i, t][:],
-                    func=RELU,
-                    bias=shift1[:, t : t + 1],
-                    scale=gain1[:, t : t + 1],
-                )
+                norm_relu(best[:, t, :] if i == 0 else h3[i][:, s, :], x3[i, t][:], t)
 
         def merge(i):
             if i >= 1:
-                nc.vector.tensor_max(out=best_act[:], in0=best_act[:], in1=h3[i][:])
+                low = SCALAR_TILES[0]
+                nc.vector.tensor_max(out=best[:, low:, :], in0=best[:, low:, :], in1=h3[i][:])
 
         def load_batch_norm(queue, g, b, m, v, label):
             loaded = const.tile([P, 4, 16], BF16, name=label + "_loaded")
@@ -201,12 +225,12 @@ def tile_p2b_xcorr_pb_kernel(tc, h2, W3, g3, b3, m3, v3, Wc1, gc1, bc1, mc1, vc1
         warm = const.tile([P, 1], F32, name="warm")
         nc.vector.memset(warm[:], 1.0)
         nc.scalar.sqrt(out=warm[:], in_=warm[:])
-        identity = const.tile([P, P], F32, name="identity")
-        make_identity(nc, identity[:])
         identity_bf = const.tile([P, P], BF16, name="identity_bf")
         make_identity(nc, identity_bf[:])
+        identity = const.tile([P, P], F32, name="identity")
+        make_identity(nc, identity[:])
         best_raw = const.tile([P, len(VECTOR_TILES), COLS], F32, name="best_raw")
-        best_act = const.tile([P, len(SCALAR_TILES), COLS], BF16, name="best_act")
+        best = const.tile([P, PACK, COLS], BF16, name="best")
 
         spread1 = start_batch_norm(bn1_loaded, "bn1")
         sign1 = const.tile([P, PACK], F32, name="sign1")
@@ -218,22 +242,32 @@ def tile_p2b_xcorr_pb_kernel(tc, h2, W3, g3, b3, m3, v3, Wc1, gc1, bc1, mc1, vc1
         gain1, shift1 = finish_batch_norm(bn1_loaded, spread1, "bn1")
         nc.vector.tensor_mul(out=size1[:], in0=gain1[:], in1=sign1[:])
 
-        regroup(0, 0, FIRST_VECTOR_COLS)
+        def regroup(i):
+            start_regroup(i)
+            vector_regroup(i)
+            scalar_regroup(i)
+
+        regroup(0)
         for t in TILE_ORDER:
             turn_weight(w3, t, sign1 if t in VECTOR_TILES else None)
         quantise(0)
         for t in TILE_ORDER:
             pack_weight(w3, t)
-        for i in range(1, GROUPED_BUFS):
-            regroup(i, 0, EARLY_VECTOR_COLS)
+        regroup(1)
+        multiply(0)
+        for i in range(2, AHEAD):
+            regroup(i)
 
         for i in range(PIECES):
-            multiply(i)
+            if i > 0:
+                multiply(i)
             quantise(i + 1)
-            merge(i - 1)
+            start_regroup(i + AHEAD)
+            merge(i - MERGE_LAG)
+            vector_regroup(i + AHEAD)
             pool_raw(i)
             activate(i)
-            regroup(i + GROUPED_BUFS)
+            scalar_regroup(i + AHEAD)
             if WC_FROM < i <= WC_FROM + PACK:
                 pack_weight(wc, i - WC_FROM - 1)
             if WC_FROM <= i < WC_FROM + PACK:
@@ -243,33 +277,28 @@ def tile_p2b_xcorr_pb_kernel(tc, h2, W3, g3, b3, m3, v3, Wc1, gc1, bc1, mc1, vc1
             if i == BN2_AT + 1:
                 gain2, shift2 = finish_batch_norm(bn2_loaded, spread2, "bn2")
 
+        for t in VECTOR_TILES:
+            norm_relu(best[:, t, :], best_raw[:, t, :], t)
+        for i in range(PIECES - MERGE_LAG, PIECES):
+            merge(i)
+        half = const.tile([P, PACK, 2 * N_SEARCH], BF16, name="half")
+        nc.vector.tensor_max(out=half[:], in0=best[:, :, : 2 * N_SEARCH], in1=best[:, :, 2 * N_SEARCH :])
         pooled = const.tile([P, N_SEARCH, PACK], BF16, name="pooled", align_bytes=64)
-        half_raw = const.tile([P, len(VECTOR_TILES), 2 * N_SEARCH], F32, name="half_raw")
-        nc.vector.tensor_max(out=half_raw[:], in0=best_raw[:, :, : 2 * N_SEARCH], in1=best_raw[:, :, 2 * N_SEARCH :])
-        top_raw = const.tile([P, len(VECTOR_TILES), N_SEARCH], F32, name="top_raw")
-        nc.vector.tensor_max(out=top_raw[:], in0=half_raw[:, :, :N_SEARCH], in1=half_raw[:, :, N_SEARCH:])
-        for s, t in enumerate(VECTOR_TILES):
-            nc.scalar.activation(
-                out=pooled[:, :, t], in_=top_raw[:, s, :], func=RELU, bias=shift1[:, t : t + 1], scale=size1[:, t : t + 1]
-            )
-        merge(PIECES - 1)
-        half_act = const.tile([P, len(SCALAR_TILES), 2 * N_SEARCH], BF16, name="half_act")
-        nc.vector.tensor_max(out=half_act[:], in0=best_act[:, :, : 2 * N_SEARCH], in1=best_act[:, :, 2 * N_SEARCH :])
         nc.vector.tensor_max(
-            out=pooled[:, :, SCALAR_TILES[0] : SCALAR_TILES[-1] + 1],
-            in0=half_act[:, :, :N_SEARCH].rearrange("p t n -> p n t"),
-            in1=half_act[:, :, N_SEARCH:].rearrange("p t n -> p n t"),
+            out=pooled[:],
+            in0=half[:, :, :N_SEARCH].rearrange("p t n -> p n t"),
+            in1=half[:, :, N_SEARCH:].rearrange("p t n -> p n t"),
         )
         p_codes = const.tile([P, N_SEARCH], U32, name="p_codes", align_bytes=64)
         p_scales = const.tile([P, N_SEARCH], U8, name="p_scales", align_bytes=64)
         nc.vector.quantize_mx(
             out=p_codes[:].bitcast(FP8X4), scales=p_scales[:], in_=pooled[:].rearrange("p n t -> p (n t)")
         )
-        xc = banks.tile([P, PACK, N_SEARCH], F32, name="xc", tag="x3")
         result = const.tile([P, PACK, N_SEARCH], F32, name="result")
         for t in range(PACK):
+            xc = banks.tile([P, N_SEARCH], F32, name="xc", tag="x3")
             nc.tensor.matmul_mx(
-                out=xc[:, t, :],
+                out=xc[:],
                 lhsT=wc[1][:, t, :].bitcast(FP8X4),
                 lhsT_scale=wc[2][:, t, :],
                 rhs=p_codes[:].bitcast(FP8X4),
@@ -277,8 +306,7 @@ def tile_p2b_xcorr_pb_kernel(tc, h2, W3, g3, b3, m3, v3, Wc1, gc1, bc1, mc1, vc1
                 start=True,
                 stop=True,
             )
-        for t in range(PACK):
             nc.scalar.activation(
-                out=result[:, t, :], in_=xc[:, t, :], func=RELU, bias=shift2[:, t : t + 1], scale=gain2[:, t : t + 1]
+                out=result[:, t, :], in_=xc[:], func=RELU, bias=shift2[:, t : t + 1], scale=gain2[:, t : t + 1]
             )
         nc.sync.dma_start(out=out[0].rearrange("(q t) n -> q t n", t=PACK), in_=result[:])

@@ -25,18 +25,24 @@ FIRST_VECTOR_COLS = 256
 RAW_BUFS = 6
 AHEAD = 3
 MERGE_LAG = 2
-VECTOR_TILES = (0, 1)
-SCALAR_TILES = (2, 3)
-TILE_ORDER = SCALAR_TILES + VECTOR_TILES
+LATE = PIECES - 4
 WC_FROM = 4
 BN2_AT = 10
 BN_EPS = 1e-5
 
 
+def vector_tiles(i):
+    return (0,) if i >= LATE else (0, 1)
+
+
+def scalar_tiles(i):
+    return (2, 3, 1) if i >= LATE else (2, 3)
+
+
 def shares(i):
     if i == 0:
         return 0, FIRST_VECTOR_COLS
-    if i <= AHEAD:
+    if i <= AHEAD + 1:
         return 0, GPSIMD_COLS
     return GPSIMD_COLS, 0
 
@@ -153,7 +159,7 @@ def tile_p2b_xcorr_pb_kernel(tc, h2, W3, g3, b3, m3, v3, Wc1, gc1, bc1, mc1, vc1
             )
 
         def multiply(i):
-            for t in TILE_ORDER:
+            for t in scalar_tiles(i) + vector_tiles(i):
                 x3[i, t] = banks.tile([P, COLS], F32, name="x3")
                 nc.tensor.matmul_mx(
                     out=x3[i, t][:],
@@ -166,7 +172,7 @@ def tile_p2b_xcorr_pb_kernel(tc, h2, W3, g3, b3, m3, v3, Wc1, gc1, bc1, mc1, vc1
                 )
 
         def pool_raw(i):
-            for t in VECTOR_TILES:
+            for t in vector_tiles(i):
                 if i == 0:
                     nc.vector.tensor_copy(out=best_raw[:, t, :], in_=x3[i, t][:])
                 else:
@@ -178,19 +184,21 @@ def tile_p2b_xcorr_pb_kernel(tc, h2, W3, g3, b3, m3, v3, Wc1, gc1, bc1, mc1, vc1
                 in_=src,
                 func=RELU,
                 bias=shift1[:, t : t + 1],
-                scale=(size1 if t in VECTOR_TILES else gain1)[:, t : t + 1],
+                scale=(size1 if t in vector_tiles(0) else gain1)[:, t : t + 1],
             )
 
         def activate(i):
             if i > 0:
-                h3[i] = work.tile([P, len(SCALAR_TILES), COLS], BF16, name="h3")
-            for s, t in enumerate(SCALAR_TILES):
-                norm_relu(best[:, t, :] if i == 0 else h3[i][:, s, :], x3[i, t][:], t)
+                h3[i] = work.tile([P, PACK - 1, COLS], BF16, name="h3")
+            for t in scalar_tiles(i):
+                if i == LATE and t in vector_tiles(0):
+                    norm_relu(best[:, t, :], best_raw[:, t, :], t)
+                norm_relu(best[:, t, :] if i == 0 else h3[i][:, t - 1, :], x3[i, t][:], t)
 
         def merge(i):
             if i >= 1:
-                low = SCALAR_TILES[0]
-                nc.vector.tensor_max(out=best[:, low:, :], in0=best[:, low:, :], in1=h3[i][:])
+                low = min(scalar_tiles(i))
+                nc.vector.tensor_max(out=best[:, low:, :], in0=best[:, low:, :], in1=h3[i][:, low - 1 :, :])
 
         def load_batch_norm(queue, g, b, m, v, label):
             loaded = const.tile([P, 4, 16], BF16, name=label + "_loaded")
@@ -208,19 +216,18 @@ def tile_p2b_xcorr_pb_kernel(tc, h2, W3, g3, b3, m3, v3, Wc1, gc1, bc1, mc1, vc1
             gain = const.tile([P, PACK], F32, name=label + "_gain")
             offset = const.tile([P, PACK], F32, name=label + "_offset")
             shift = const.tile([P, PACK], F32, name=label + "_shift")
-            nc.vector.reciprocal(out=spread[:], in_=spread[:])
-            nc.vector.tensor_mul(out=gain[:], in0=loaded[:, 0, 0:PACK], in1=spread[:])
-            nc.vector.tensor_mul(out=offset[:], in0=gain[:], in1=loaded[:, 2, 0:PACK])
-            nc.vector.tensor_sub(out=shift[:], in0=loaded[:, 1, 0:PACK], in1=offset[:])
-            return gain, shift
+            return gain, shift, (
+                lambda: nc.vector.reciprocal(out=spread[:], in_=spread[:]),
+                lambda: nc.vector.tensor_mul(out=gain[:], in0=loaded[:, 0, 0:PACK], in1=spread[:]),
+                lambda: nc.vector.tensor_mul(out=offset[:], in0=gain[:], in1=loaded[:, 2, 0:PACK]),
+                lambda: nc.vector.tensor_sub(out=shift[:], in0=loaded[:, 1, 0:PACK], in1=offset[:]),
+            )
 
         bn1_loaded = load_batch_norm(nc.sync, g3, b3, m3, v3, "bn1")
         load(0)
         w3 = load_weight(W3, "w3")
         for i in range(1, RAW_BUFS):
             load(i)
-        wc = load_weight(Wc1, "wc")
-        bn2_loaded = load_batch_norm(nc.sync, gc1, bc1, mc1, vc1, "bn2")
 
         warm = const.tile([P, 1], F32, name="warm")
         nc.vector.memset(warm[:], 1.0)
@@ -229,7 +236,7 @@ def tile_p2b_xcorr_pb_kernel(tc, h2, W3, g3, b3, m3, v3, Wc1, gc1, bc1, mc1, vc1
         make_identity(nc, identity_bf[:])
         identity = const.tile([P, P], F32, name="identity")
         make_identity(nc, identity[:])
-        best_raw = const.tile([P, len(VECTOR_TILES), COLS], F32, name="best_raw")
+        best_raw = const.tile([P, len(vector_tiles(0)), COLS], F32, name="best_raw")
         best = const.tile([P, PACK, COLS], BF16, name="best")
 
         spread1 = start_batch_norm(bn1_loaded, "bn1")
@@ -239,7 +246,9 @@ def tile_p2b_xcorr_pb_kernel(tc, h2, W3, g3, b3, m3, v3, Wc1, gc1, bc1, mc1, vc1
             out=sign1[:], in0=bn1_loaded[:, 0, 0:PACK], scalar1=0.0, scalar2=2.0, op0=ALU.is_ge, op1=ALU.mult
         )
         nc.vector.tensor_scalar_add(out=sign1[:], in0=sign1[:], scalar1=-1.0)
-        gain1, shift1 = finish_batch_norm(bn1_loaded, spread1, "bn1")
+        gain1, shift1, bn1_steps = finish_batch_norm(bn1_loaded, spread1, "bn1")
+        for step in bn1_steps:
+            step()
         nc.vector.tensor_mul(out=size1[:], in0=gain1[:], in1=sign1[:])
 
         def regroup(i):
@@ -248,15 +257,17 @@ def tile_p2b_xcorr_pb_kernel(tc, h2, W3, g3, b3, m3, v3, Wc1, gc1, bc1, mc1, vc1
             scalar_regroup(i)
 
         regroup(0)
-        for t in TILE_ORDER:
-            turn_weight(w3, t, sign1 if t in VECTOR_TILES else None)
+        for t in scalar_tiles(0) + vector_tiles(0):
+            turn_weight(w3, t, sign1 if t in vector_tiles(0) else None)
         quantise(0)
-        for t in TILE_ORDER:
+        for t in scalar_tiles(0) + vector_tiles(0):
             pack_weight(w3, t)
         regroup(1)
         multiply(0)
         for i in range(2, AHEAD):
             regroup(i)
+        wc = load_weight(Wc1, "wc")
+        bn2_loaded = load_batch_norm(nc.sync, gc1, bc1, mc1, vc1, "bn2")
 
         for i in range(PIECES):
             if i > 0:
@@ -274,10 +285,11 @@ def tile_p2b_xcorr_pb_kernel(tc, h2, W3, g3, b3, m3, v3, Wc1, gc1, bc1, mc1, vc1
                 turn_weight(wc, i - WC_FROM, None)
             if i == BN2_AT:
                 spread2 = start_batch_norm(bn2_loaded, "bn2")
-            if i == BN2_AT + 1:
-                gain2, shift2 = finish_batch_norm(bn2_loaded, spread2, "bn2")
+                gain2, shift2, bn2_steps = finish_batch_norm(bn2_loaded, spread2, "bn2")
+            if BN2_AT < i <= BN2_AT + len(bn2_steps):
+                bn2_steps[i - BN2_AT - 1]()
 
-        for t in VECTOR_TILES:
+        for t in vector_tiles(PIECES - 1):
             norm_relu(best[:, t, :], best_raw[:, t, :], t)
         for i in range(PIECES - MERGE_LAG, PIECES):
             merge(i)

@@ -25,7 +25,7 @@ FIRST_VECTOR_COLS = 256
 RAW_BUFS = 6
 AHEAD = 3
 MERGE_LAG = 2
-LATE = PIECES - 4
+LATE = PIECES - 2
 WC_FROM = 4
 BN2_AT = 10
 BN_EPS = 1e-5

@@ -321,4 +321,7 @@ def tile_p2b_xcorr_pb_kernel(tc, h2, W3, g3, b3, m3, v3, Wc1, gc1, bc1, mc1, vc1
             nc.scalar.activation(
                 out=result[:, t, :], in_=xc[:], func=RELU, bias=shift2[:, t : t + 1], scale=gain2[:, t : t + 1]
             )
-        nc.sync.dma_start(out=out[0].rearrange("(q t) n -> q t n", t=PACK), in_=result[:])
+            if t % 2 == 1:
+                nc.sync.dma_start(
+                    out=out[0].rearrange("(q t) n -> q t n", t=PACK)[:, t - 1 : t + 1, :], in_=result[:, t - 1 : t + 1, :]
+                )

@@ -137,12 +137,8 @@ def tile_p2b_xcorr_pb_kernel(tc, h2, W3, g3, b3, m3, v3, Wc1, gc1, bc1, mc1, vc1
             w_scales = const.tile([P, PACK, P], U8, name=label + "_scales", align_bytes=64)
             return w_sb, w_codes, w_scales
 
-        def turn_weight(weight, t, row_sign):
+        def turn_weight(weight, t):
             rows = weight[0][:, t, :]
-            if row_sign is not None:
-                signed = work.tile([P, H], BF16, name="signed")
-                nc.vector.tensor_scalar_mul(out=signed[:], in0=rows, scalar1=row_sign[:, t : t + 1])
-                rows = signed[:]
             words = rows.bitcast(F32).rearrange("q (p u) -> q u p", u=2)
             turned = banks.tile([P, 2, P], F32, name="turned", tag="x3")
             for u in range(2):
@@ -174,26 +170,27 @@ def tile_p2b_xcorr_pb_kernel(tc, h2, W3, g3, b3, m3, v3, Wc1, gc1, bc1, mc1, vc1
         def pool_raw(i):
             for t in vector_tiles(i):
                 if i == 0:
-                    nc.vector.tensor_copy(out=best_raw[:, t, :], in_=x3[i, t][:])
+                    nc.vector.tensor_scalar_mul(out=best_raw[:, t, :], in0=x3[i, t][:], scalar1=sign1[:, t : t + 1])
                 else:
-                    nc.vector.tensor_max(out=best_raw[:, t, :], in0=x3[i, t][:], in1=best_raw[:, t, :])
+                    nc.vector.scalar_tensor_tensor(
+                        out=best_raw[:, t, :],
+                        in0=x3[i, t][:],
+                        scalar=sign1[:, t : t + 1],
+                        in1=best_raw[:, t, :],
+                        op0=ALU.mult,
+                        op1=ALU.max,
+                    )
 
-        def norm_relu(dst, src, t):
-            nc.scalar.activation(
-                out=dst,
-                in_=src,
-                func=RELU,
-                bias=shift1[:, t : t + 1],
-                scale=(size1 if t in vector_tiles(0) else gain1)[:, t : t + 1],
-            )
+        def norm_relu(dst, src, t, gain):
+            nc.scalar.activation(out=dst, in_=src, func=RELU, bias=shift1[:, t : t + 1], scale=gain[:, t : t + 1])
 
         def activate(i):
             if i > 0:
                 h3[i] = work.tile([P, PACK - 1, COLS], BF16, name="h3")
             for t in scalar_tiles(i):
                 if i == LATE and t in vector_tiles(0):
-                    norm_relu(best[:, t, :], best_raw[:, t, :], t)
-                norm_relu(best[:, t, :] if i == 0 else h3[i][:, t - 1, :], x3[i, t][:], t)
+                    norm_relu(best[:, t, :], best_raw[:, t, :], t, size1)
+                norm_relu(best[:, t, :] if i == 0 else h3[i][:, t - 1, :], x3[i, t][:], t, gain1)
 
         def merge(i):
             if i >= 1:
@@ -258,7 +255,7 @@ def tile_p2b_xcorr_pb_kernel(tc, h2, W3, g3, b3, m3, v3, Wc1, gc1, bc1, mc1, vc1
 
         regroup(0)
         for t in scalar_tiles(0) + vector_tiles(0):
-            turn_weight(w3, t, sign1 if t in vector_tiles(0) else None)
+            turn_weight(w3, t)
         quantise(0)
         for t in scalar_tiles(0) + vector_tiles(0):
             pack_weight(w3, t)
@@ -282,7 +279,7 @@ def tile_p2b_xcorr_pb_kernel(tc, h2, W3, g3, b3, m3, v3, Wc1, gc1, bc1, mc1, vc1
             if WC_FROM < i <= WC_FROM + PACK:
                 pack_weight(wc, i - WC_FROM - 1)
             if WC_FROM <= i < WC_FROM + PACK:
-                turn_weight(wc, i - WC_FROM, None)
+                turn_weight(wc, i - WC_FROM)
             if i == BN2_AT:
                 spread2 = start_batch_norm(bn2_loaded, "bn2")
                 gain2, shift2, bn2_steps = finish_batch_norm(bn2_loaded, spread2, "bn2")
@@ -290,7 +287,7 @@ def tile_p2b_xcorr_pb_kernel(tc, h2, W3, g3, b3, m3, v3, Wc1, gc1, bc1, mc1, vc1
                 bn2_steps[i - BN2_AT - 1]()
 
         for t in vector_tiles(PIECES - 1):
-            norm_relu(best[:, t, :], best_raw[:, t, :], t)
+            norm_relu(best[:, t, :], best_raw[:, t, :], t, size1)
         for i in range(PIECES - MERGE_LAG, PIECES):
             merge(i)
         half = const.tile([P, PACK, 2 * N_SEARCH], BF16, name="half")

@@ -170,27 +170,27 @@ def tile_p2b_xcorr_pb_kernel(tc, h2, W3, g3, b3, m3, v3, Wc1, gc1, bc1, mc1, vc1
         def pool_raw(i):
             for t in vector_tiles(i):
                 if i == 0:
-                    nc.vector.tensor_scalar_mul(out=best_raw[:, t, :], in0=x3[i, t][:], scalar1=sign1[:, t : t + 1])
+                    nc.vector.tensor_scalar_mul(out=best_raw[:, t, :], in0=x3[i, t][:], scalar1=gain1[:, t : t + 1])
                 else:
                     nc.vector.scalar_tensor_tensor(
                         out=best_raw[:, t, :],
                         in0=x3[i, t][:],
-                        scalar=sign1[:, t : t + 1],
+                        scalar=gain1[:, t : t + 1],
                         in1=best_raw[:, t, :],
                         op0=ALU.mult,
                         op1=ALU.max,
                     )
 
         def norm_relu(dst, src, t, gain):
-            nc.scalar.activation(out=dst, in_=src, func=RELU, bias=shift1[:, t : t + 1], scale=gain[:, t : t + 1])
+            nc.scalar.activation(out=dst, in_=src, func=RELU, bias=shift1[:, t : t + 1], scale=gain)
 
         def activate(i):
             if i > 0:
                 h3[i] = work.tile([P, PACK - 1, COLS], BF16, name="h3")
             for t in scalar_tiles(i):
                 if i == LATE and t in vector_tiles(0):
-                    norm_relu(best[:, t, :], best_raw[:, t, :], t, size1)
-                norm_relu(best[:, t, :] if i == 0 else h3[i][:, t - 1, :], x3[i, t][:], t, gain1)
+                    norm_relu(best[:, t, :], best_raw[:, t, :], t, 1.0)
+                norm_relu(best[:, t, :] if i == 0 else h3[i][:, t - 1, :], x3[i, t][:], t, gain1[:, t : t + 1])
 
         def merge(i):
             if i >= 1:
@@ -220,9 +220,9 @@ def tile_p2b_xcorr_pb_kernel(tc, h2, W3, g3, b3, m3, v3, Wc1, gc1, bc1, mc1, vc1
                 lambda: nc.vector.tensor_sub(out=shift[:], in0=loaded[:, 1, 0:PACK], in1=offset[:]),
             )
 
-        bn1_loaded = load_batch_norm(nc.sync, g3, b3, m3, v3, "bn1")
         load(0)
         w3 = load_weight(W3, "w3")
+        bn1_loaded = load_batch_norm(nc.sync, g3, b3, m3, v3, "bn1")
         for i in range(1, RAW_BUFS):
             load(i)
 
@@ -236,28 +236,19 @@ def tile_p2b_xcorr_pb_kernel(tc, h2, W3, g3, b3, m3, v3, Wc1, gc1, bc1, mc1, vc1
         best_raw = const.tile([P, len(vector_tiles(0)), COLS], F32, name="best_raw")
         best = const.tile([P, PACK, COLS], BF16, name="best")
 
-        spread1 = start_batch_norm(bn1_loaded, "bn1")
-        sign1 = const.tile([P, PACK], F32, name="sign1")
-        size1 = const.tile([P, PACK], F32, name="size1")
-        nc.vector.tensor_scalar(
-            out=sign1[:], in0=bn1_loaded[:, 0, 0:PACK], scalar1=0.0, scalar2=2.0, op0=ALU.is_ge, op1=ALU.mult
-        )
-        nc.vector.tensor_scalar_add(out=sign1[:], in0=sign1[:], scalar1=-1.0)
-        gain1, shift1, bn1_steps = finish_batch_norm(bn1_loaded, spread1, "bn1")
-        for step in bn1_steps:
-            step()
-        nc.vector.tensor_mul(out=size1[:], in0=gain1[:], in1=sign1[:])
-
         def regroup(i):
             start_regroup(i)
             vector_regroup(i)
             scalar_regroup(i)
 
         regroup(0)
+        spread1 = start_batch_norm(bn1_loaded, "bn1")
+        gain1, shift1, bn1_steps = finish_batch_norm(bn1_loaded, spread1, "bn1")
         for t in scalar_tiles(0) + vector_tiles(0):
             turn_weight(w3, t)
         quantise(0)
-        for t in scalar_tiles(0) + vector_tiles(0):
+        for t, step in zip(scalar_tiles(0) + vector_tiles(0), bn1_steps):
+            step()
             pack_weight(w3, t)
         regroup(1)
         multiply(0)
@@ -287,7 +278,7 @@ def tile_p2b_xcorr_pb_kernel(tc, h2, W3, g3, b3, m3, v3, Wc1, gc1, bc1, mc1, vc1
                 bn2_steps[i - BN2_AT - 1]()
 
         for t in vector_tiles(PIECES - 1):
-            norm_relu(best[:, t, :], best_raw[:, t, :], t, size1)
+            norm_relu(best[:, t, :], best_raw[:, t, :], t, 1.0)
         for i in range(PIECES - MERGE_LAG, PIECES):
             merge(i)
         half = const.tile([P, PACK, 2 * N_SEARCH], BF16, name="half")

@@ -27,7 +27,6 @@ AHEAD = 3
 MERGE_LAG = 2
 LATE = PIECES - 2
 WC_FROM = 4
-BN2_AT = 10
 BN_EPS = 1e-5
 
 
@@ -81,9 +80,10 @@ def tile_p2b_xcorr_pb_kernel(tc, h2, W3, g3, b3, m3, v3, Wc1, gc1, bc1, mc1, vc1
             gpsimd_cols = shares(i)[0]
             grouped[i] = regrouped.tile([P, COLS, PACK], BF16, name="grouped", align_bytes=64)
             if gpsimd_cols:
+                mine = slice(TENSOR_COLS, TENSOR_COLS + gpsimd_cols)
                 nc.gpsimd.tensor_scalar(
-                    out=grouped[i][:, :gpsimd_cols, :],
-                    in0=raw[i][:, :, :gpsimd_cols].rearrange("p j w -> p w j"),
+                    out=grouped[i][:, mine, :],
+                    in0=raw[i][:, :, mine].rearrange("p j w -> p w j"),
                     scalar1=1.0,
                     scalar2=0.0,
                     op0=ALU.mult,
@@ -94,7 +94,7 @@ def tile_p2b_xcorr_pb_kernel(tc, h2, W3, g3, b3, m3, v3, Wc1, gc1, bc1, mc1, vc1
                 nc.tensor.matmul(
                     out=passed[i][:, :, 2 * u : 2 * u + 2],
                     lhsT=identity_bf[:],
-                    rhs=raw[i][:, 2 * u : 2 * u + 2, gpsimd_cols : gpsimd_cols + TENSOR_COLS].rearrange("p j w -> p w j"),
+                    rhs=raw[i][:, 2 * u : 2 * u + 2, :TENSOR_COLS].rearrange("p j w -> p w j"),
                     start=True,
                     stop=True,
                 )
@@ -102,8 +102,8 @@ def tile_p2b_xcorr_pb_kernel(tc, h2, W3, g3, b3, m3, v3, Wc1, gc1, bc1, mc1, vc1
         def runs(i):
             dst = grouped[i][:].rearrange("p (c r) j -> p c j r", r=RUN)
             src = raw[i][:].rearrange("p j (c r) -> p c j r", r=RUN)
-            first = (shares(i)[0] + TENSOR_COLS) // RUN
-            return dst, src, first, first + shares(i)[1] // RUN
+            first = TENSOR_COLS // RUN
+            return dst, src, first, first + sum(shares(i)) // RUN
 
         def vector_regroup(i):
             if i < PIECES and shares(i)[1]:
@@ -113,9 +113,10 @@ def tile_p2b_xcorr_pb_kernel(tc, h2, W3, g3, b3, m3, v3, Wc1, gc1, bc1, mc1, vc1
         def scalar_regroup(i):
             if i >= PIECES:
                 return
-            gpsimd_cols = shares(i)[0]
-            nc.scalar.copy(out=grouped[i][:, gpsimd_cols : gpsimd_cols + TENSOR_COLS, :], in_=passed[i][:])
+            nc.scalar.copy(out=grouped[i][:, :TENSOR_COLS, :], in_=passed[i][:])
             dst, src, first, cut = runs(i)
+            if shares(i)[0]:
+                cut -= 1
             nc.scalar.copy(out=dst[:, cut:], in_=src[:, cut:])
             load(i + RAW_BUFS)
 
@@ -137,21 +138,23 @@ def tile_p2b_xcorr_pb_kernel(tc, h2, W3, g3, b3, m3, v3, Wc1, gc1, bc1, mc1, vc1
             w_scales = const.tile([P, PACK, P], U8, name=label + "_scales", align_bytes=64)
             return w_sb, w_codes, w_scales
 
-        def turn_weight(weight, t):
-            rows = weight[0][:, t, :]
-            words = rows.bitcast(F32).rearrange("q (p u) -> q u p", u=2)
-            turned = banks.tile([P, 2, P], F32, name="turned", tag="x3")
-            for u in range(2):
-                nc.tensor.transpose(turned[:, u, :], words[:, u, :], identity[:])
-            w_grouped[t] = work.tile([P, H], BF16, name="w_grouped", align_bytes=64)
+        def turn_weight(weight, t, count):
+            turned = banks.tile([P, count, 2, P], F32, name="turned", tag="x3")
+            for k in range(count):
+                words = weight[0][:, t + k, :].bitcast(F32).rearrange("q (p u) -> q u p", u=2)
+                for u in range(2):
+                    nc.tensor.transpose(turned[:, k, u, :], words[:, u, :], identity[:])
+            w_grouped[t] = work.tile([P, count * H], BF16, name="w_grouped", align_bytes=64)
             nc.scalar.copy(
-                out=w_grouped[t][:].bitcast(F32).rearrange("p (q u) -> p q u", u=2),
-                in_=turned[:].rearrange("p u q -> p q u"),
+                out=w_grouped[t][:].bitcast(F32).rearrange("p (k q u) -> p k q u", k=count, u=2),
+                in_=turned[:].rearrange("p k u q -> p k q u"),
             )
 
-        def pack_weight(weight, t):
+        def pack_weight(weight, t, count):
             nc.vector.quantize_mx(
-                out=weight[1][:, t, :].bitcast(FP8X4), scales=weight[2][:, t, :], in_=w_grouped[t][:]
+                out=weight[1][:, t : t + count, :].rearrange("p k q -> p (k q)").bitcast(FP8X4),
+                scales=weight[2][:, t : t + count, :].rearrange("p k q -> p (k q)"),
+                in_=w_grouped[t][:],
             )
 
         def multiply(i):
@@ -220,6 +223,20 @@ def tile_p2b_xcorr_pb_kernel(tc, h2, W3, g3, b3, m3, v3, Wc1, gc1, bc1, mc1, vc1
                 lambda: nc.vector.tensor_sub(out=shift[:], in0=loaded[:, 1, 0:PACK], in1=offset[:]),
             )
 
+        def gpsimd_batch_norm(loaded, label):
+            spread = const.tile([P, PACK], F32, name=label + "_spread")
+            gain = const.tile([P, PACK], F32, name=label + "_gain")
+            offset = const.tile([P, PACK], F32, name=label + "_offset")
+            shift = const.tile([P, PACK], F32, name=label + "_shift")
+            nc.gpsimd.tensor_scalar(
+                out=spread[:], in0=loaded[:, 3, 0:PACK], scalar1=1.0, scalar2=BN_EPS, op0=ALU.mult, op1=ALU.add
+            )
+            nc.gpsimd.tensor_tensor(out=spread[:], in0=spread[:], in1=minus_half[:], op=ALU.pow)
+            nc.gpsimd.tensor_tensor(out=gain[:], in0=loaded[:, 0, 0:PACK], in1=spread[:], op=ALU.mult)
+            nc.gpsimd.tensor_tensor(out=offset[:], in0=gain[:], in1=loaded[:, 2, 0:PACK], op=ALU.mult)
+            nc.gpsimd.tensor_tensor(out=shift[:], in0=loaded[:, 1, 0:PACK], in1=offset[:], op=ALU.subtract)
+            return gain, shift
+
         load(0)
         w3 = load_weight(W3, "w3")
         bn1_loaded = load_batch_norm(nc.sync, g3, b3, m3, v3, "bn1")
@@ -229,6 +246,8 @@ def tile_p2b_xcorr_pb_kernel(tc, h2, W3, g3, b3, m3, v3, Wc1, gc1, bc1, mc1, vc1
         warm = const.tile([P, 1], F32, name="warm")
         nc.vector.memset(warm[:], 1.0)
         nc.scalar.sqrt(out=warm[:], in_=warm[:])
+        minus_half = const.tile([P, PACK], F32, name="minus_half")
+        nc.vector.memset(minus_half[:], -0.5)
         identity_bf = const.tile([P, P], BF16, name="identity_bf")
         make_identity(nc, identity_bf[:])
         identity = const.tile([P, P], F32, name="identity")
@@ -245,11 +264,11 @@ def tile_p2b_xcorr_pb_kernel(tc, h2, W3, g3, b3, m3, v3, Wc1, gc1, bc1, mc1, vc1
         spread1 = start_batch_norm(bn1_loaded, "bn1")
         gain1, shift1, bn1_steps = finish_batch_norm(bn1_loaded, spread1, "bn1")
         for t in scalar_tiles(0) + vector_tiles(0):
-            turn_weight(w3, t)
+            turn_weight(w3, t, 1)
         quantise(0)
         for t, step in zip(scalar_tiles(0) + vector_tiles(0), bn1_steps):
             step()
-            pack_weight(w3, t)
+            pack_weight(w3, t, 1)
         regroup(1)
         multiply(0)
         for i in range(2, AHEAD):
@@ -267,15 +286,12 @@ def tile_p2b_xcorr_pb_kernel(tc, h2, W3, g3, b3, m3, v3, Wc1, gc1, bc1, mc1, vc1
             pool_raw(i)
             activate(i)
             scalar_regroup(i + AHEAD)
-            if WC_FROM < i <= WC_FROM + PACK:
-                pack_weight(wc, i - WC_FROM - 1)
-            if WC_FROM <= i < WC_FROM + PACK:
-                turn_weight(wc, i - WC_FROM)
-            if i == BN2_AT:
-                spread2 = start_batch_norm(bn2_loaded, "bn2")
-                gain2, shift2, bn2_steps = finish_batch_norm(bn2_loaded, spread2, "bn2")
-            if BN2_AT < i <= BN2_AT + len(bn2_steps):
-                bn2_steps[i - BN2_AT - 1]()
+            if i in (WC_FROM + 1, WC_FROM + 2):
+                pack_weight(wc, 2 * (i - WC_FROM - 1), 2)
+            if i in (WC_FROM, WC_FROM + 1):
+                turn_weight(wc, 2 * (i - WC_FROM), 2)
+
+        gain2, shift2 = gpsimd_batch_norm(bn2_loaded, "bn2")
 
         for t in vector_tiles(PIECES - 1):
             norm_relu(best[:, t, :], best_raw[:, t, :], t, 1.0)

@@ -90,11 +90,13 @@ def tile_p2b_xcorr_pb_kernel(tc, h2, W3, g3, b3, m3, v3, Wc1, gc1, bc1, mc1, vc1
                     op1=ALU.add,
                 )
             passed[i] = passing.tile([P, TENSOR_COLS, PACK], BF16, name="passed")
+            dst = passed[i][:].rearrange("p (c r) j -> p c j r", r=RUN)
+            src = raw[i][:, :, :TENSOR_COLS].rearrange("p j (c r) -> p c j r", r=RUN)
             for u in range(PACK // 2):
                 nc.tensor.matmul(
-                    out=passed[i][:, :, 2 * u : 2 * u + 2],
+                    out=dst[:, :, 2 * u : 2 * u + 2, :],
                     lhsT=identity_bf[:],
-                    rhs=raw[i][:, 2 * u : 2 * u + 2, :TENSOR_COLS].rearrange("p j w -> p w j"),
+                    rhs=src[:, :, 2 * u : 2 * u + 2, :],
                     start=True,
                     stop=True,
                 )

@@ -20,12 +20,14 @@ COLS = 512
 PIECES = PAIRS // COLS
 RUN = 4
 GPSIMD_COLS = 192
-TENSOR_COLS = 204
-FIRST_VECTOR_COLS = 256
+TENSOR_COLS = 208
+HEAD_TENSOR_COLS = 208
+FIRST_TENSOR_COLS = 104
+HEAD_VECTOR_COLS = 192
 RAW_BUFS = 6
 AHEAD = 3
 MERGE_LAG = 2
-LATE = PIECES - 2
+LATE = PIECES - 3
 WC_FROM = 4
 BN_EPS = 1e-5
 
@@ -40,10 +42,10 @@ def scalar_tiles(i):
 
 def shares(i):
     if i == 0:
-        return 0, FIRST_VECTOR_COLS
-    if i <= AHEAD + 1:
-        return 0, GPSIMD_COLS
-    return GPSIMD_COLS, 0
+        return FIRST_TENSOR_COLS, 0, COLS - FIRST_TENSOR_COLS
+    if i <= AHEAD:
+        return HEAD_TENSOR_COLS, 0, HEAD_VECTOR_COLS
+    return TENSOR_COLS, GPSIMD_COLS, 0
 
 
 def tile_p2b_xcorr_pb_kernel(tc, h2, W3, g3, b3, m3, v3, Wc1, gc1, bc1, mc1, vc1, out):
@@ -77,10 +79,10 @@ def tile_p2b_xcorr_pb_kernel(tc, h2, W3, g3, b3, m3, v3, Wc1, gc1, bc1, mc1, vc1
         def start_regroup(i):
             if i >= PIECES:
                 return
-            gpsimd_cols = shares(i)[0]
+            tensor_cols, gpsimd_cols, vector_cols = shares(i)
             grouped[i] = regrouped.tile([P, COLS, PACK], BF16, name="grouped", align_bytes=64)
             if gpsimd_cols:
-                mine = slice(TENSOR_COLS, TENSOR_COLS + gpsimd_cols)
+                mine = slice(tensor_cols, tensor_cols + gpsimd_cols)
                 nc.gpsimd.tensor_scalar(
                     out=grouped[i][:, mine, :],
                     in0=raw[i][:, :, mine].rearrange("p j w -> p w j"),
@@ -89,9 +91,9 @@ def tile_p2b_xcorr_pb_kernel(tc, h2, W3, g3, b3, m3, v3, Wc1, gc1, bc1, mc1, vc1
                     op0=ALU.mult,
                     op1=ALU.add,
                 )
-            passed[i] = passing.tile([P, TENSOR_COLS, PACK], BF16, name="passed")
+            passed[i] = passing.tile([P, tensor_cols, PACK], BF16, name="passed")
             dst = passed[i][:].rearrange("p (c r) j -> p c j r", r=RUN)
-            src = raw[i][:, :, :TENSOR_COLS].rearrange("p j (c r) -> p c j r", r=RUN)
+            src = raw[i][:, :, :tensor_cols].rearrange("p j (c r) -> p c j r", r=RUN)
             for u in range(PACK // 2):
                 nc.tensor.matmul(
                     out=dst[:, :, 2 * u : 2 * u + 2, :],
@@ -104,22 +106,22 @@ def tile_p2b_xcorr_pb_kernel(tc, h2, W3, g3, b3, m3, v3, Wc1, gc1, bc1, mc1, vc1
         def runs(i):
             dst = grouped[i][:].rearrange("p (c r) j -> p c j r", r=RUN)
             src = raw[i][:].rearrange("p j (c r) -> p c j r", r=RUN)
-            first = TENSOR_COLS // RUN
-            return dst, src, first, first + sum(shares(i)) // RUN
+            return dst, src, shares(i)[0] // RUN, sum(shares(i)) // RUN
 
         def vector_regroup(i):
-            if i < PIECES and shares(i)[1]:
+            if i < PIECES and shares(i)[2]:
                 dst, src, first, cut = runs(i)
                 nc.vector.tensor_copy(out=dst[:, first:cut], in_=src[:, first:cut])
 
         def scalar_regroup(i):
             if i >= PIECES:
                 return
-            nc.scalar.copy(out=grouped[i][:, :TENSOR_COLS, :], in_=passed[i][:])
+            nc.scalar.copy(out=grouped[i][:, : shares(i)[0], :], in_=passed[i][:])
             dst, src, first, cut = runs(i)
-            if shares(i)[0]:
+            if shares(i)[1]:
                 cut -= 1
-            nc.scalar.copy(out=dst[:, cut:], in_=src[:, cut:])
+            if cut < COLS // RUN:
+                nc.scalar.copy(out=dst[:, cut:], in_=src[:, cut:])
             load(i + RAW_BUFS)
 
         def quantise(i):
@@ -263,18 +265,23 @@ def tile_p2b_xcorr_pb_kernel(tc, h2, W3, g3, b3, m3, v3, Wc1, gc1, bc1, mc1, vc1
             scalar_regroup(i)
 
         regroup(0)
+        quantise(0)
+        first_tiles = scalar_tiles(0) + vector_tiles(0)
+        for t in first_tiles[:2]:
+            turn_weight(w3, t, 1)
         spread1 = start_batch_norm(bn1_loaded, "bn1")
         gain1, shift1, bn1_steps = finish_batch_norm(bn1_loaded, spread1, "bn1")
-        for t in scalar_tiles(0) + vector_tiles(0):
+        for t in first_tiles[2:]:
             turn_weight(w3, t, 1)
-        quantise(0)
-        for t, step in zip(scalar_tiles(0) + vector_tiles(0), bn1_steps):
+        for t in first_tiles[:2]:
+            pack_weight(w3, t, 1)
+        for t, step in zip(first_tiles[2:], bn1_steps):
             step()
             pack_weight(w3, t, 1)
-        regroup(1)
-        multiply(0)
-        for i in range(2, AHEAD):
+        for i in range(1, AHEAD):
             regroup(i)
+            bn1_steps[i + 1]()
+        multiply(0)
         wc = load_weight(Wc1, "wc")
         bn2_loaded = load_batch_norm(nc.sync, gc1, bc1, mc1, vc1, "bn2")
 

@@ -19,7 +19,7 @@ N_SEARCH = 128
 COLS = 512
 PIECES = PAIRS // COLS
 RUN = 4
-GPSIMD_COLS = 192
+GPSIMD_COLS = 176
 TENSOR_COLS = 208
 HEAD_TENSOR_COLS = 208
 FIRST_TENSOR_COLS = 104

@@ -20,13 +20,14 @@ COLS = 512
 PIECES = PAIRS // COLS
 RUN = 4
 GPSIMD_COLS = 176
+EARLY_GPSIMD_COLS = 152
 TENSOR_COLS = 208
 HEAD_TENSOR_COLS = 208
 FIRST_TENSOR_COLS = 104
 HEAD_VECTOR_COLS = 192
 RAW_BUFS = 6
 AHEAD = 3
-MERGE_LAG = 2
+MERGE_LAG = 1
 LATE = PIECES - 3
 WC_FROM = 4
 BN_EPS = 1e-5
@@ -45,6 +46,8 @@ def shares(i):
         return FIRST_TENSOR_COLS, 0, COLS - FIRST_TENSOR_COLS
     if i <= AHEAD:
         return HEAD_TENSOR_COLS, 0, HEAD_VECTOR_COLS
+    if i <= AHEAD + 2:
+        return TENSOR_COLS, EARLY_GPSIMD_COLS, 0
     return TENSOR_COLS, GPSIMD_COLS, 0
 
 

import concourse.mybir as mybir
from concourse.masks import make_identity

FLOPS = 2 * 512 * 512 * (128 * 128) + 2 * 512 * 512 * 128

BF16 = mybir.dt.bfloat16
F32 = mybir.dt.float32
U32 = mybir.dt.uint32
U8 = mybir.dt.uint8
FP8X4 = mybir.dt.float8_e4m3fn_x4
RELU = mybir.ActivationFunctionType.Relu
ALU = mybir.AluOpType

P = 128
PACK = 4
H = P * PACK
PAIRS = 128 * 128
N_SEARCH = 128
COLS = 512
PIECES = PAIRS // COLS
RUN = 4
GPSIMD_COLS = 176
EARLY_GPSIMD_COLS = 152
TENSOR_COLS = 208
HEAD_TENSOR_COLS = 208
FIRST_TENSOR_COLS = 104
HEAD_VECTOR_COLS = 192
RAW_BUFS = 6
AHEAD = 3
MERGE_LAG = 1
LATE = PIECES - 3
WC_FROM = 4
BN_EPS = 1e-5


def vector_tiles(i):
    return (0,) if i >= LATE else (0, 1)


def scalar_tiles(i):
    return (2, 3, 1) if i >= LATE else (2, 3)


def shares(i):
    if i == 0:
        return FIRST_TENSOR_COLS, 0, COLS - FIRST_TENSOR_COLS
    if i <= AHEAD:
        return HEAD_TENSOR_COLS, 0, HEAD_VECTOR_COLS
    if i <= AHEAD + 2:
        return TENSOR_COLS, EARLY_GPSIMD_COLS, 0
    return TENSOR_COLS, GPSIMD_COLS, 0


def tile_p2b_xcorr_pb_kernel(tc, h2, W3, g3, b3, m3, v3, Wc1, gc1, bc1, mc1, vc1, out):
    nc = tc.nc
    h2_rows = h2[0].rearrange("(p j) m n -> p j (m n)", j=PACK)

    with (
        tc.tile_pool(name="const", bufs=1) as const,
        tc.tile_pool(name="raw", bufs=RAW_BUFS) as raw_pool,
        tc.tile_pool(name="regrouped", bufs=AHEAD) as regrouped,
        tc.tile_pool(name="work", bufs=4) as work,
        tc.tile_pool(name="packed", bufs=PIECES) as packed,
        tc.psum_pool(name="banks", bufs=6) as banks,
        tc.psum_pool(name="passing", bufs=2) as passing,
        tc.manual_schedule(),
    ):
        raw = {}
        grouped = {}
        passed = {}
        codes = {}
        scales = {}
        x3 = {}
        h3 = {}
        w_grouped = {}

        def load(i):
            if i < PIECES:
                raw[i] = raw_pool.tile([P, PACK, COLS], BF16, name="raw")
                nc.sync.dma_start(out=raw[i][:], in_=h2_rows[:, :, i * COLS : (i + 1) * COLS])

        def start_regroup(i):
            if i >= PIECES:
                return
            tensor_cols, gpsimd_cols, vector_cols = shares(i)
            grouped[i] = regrouped.tile([P, COLS, PACK], BF16, name="grouped", align_bytes=64)
            if gpsimd_cols:
                mine = slice(tensor_cols, tensor_cols + gpsimd_cols)
                nc.gpsimd.tensor_scalar(
                    out=grouped[i][:, mine, :],
                    in0=raw[i][:, :, mine].rearrange("p j w -> p w j"),
                    scalar1=1.0,
                    scalar2=0.0,
                    op0=ALU.mult,
                    op1=ALU.add,
                )
            passed[i] = passing.tile([P, tensor_cols, PACK], BF16, name="passed")
            dst = passed[i][:].rearrange("p (c r) j -> p c j r", r=RUN)
            src = raw[i][:, :, :tensor_cols].rearrange("p j (c r) -> p c j r", r=RUN)
            for u in range(PACK // 2):
                nc.tensor.matmul(
                    out=dst[:, :, 2 * u : 2 * u + 2, :],
                    lhsT=identity_bf[:],
                    rhs=src[:, :, 2 * u : 2 * u + 2, :],
                    start=True,
                    stop=True,
                )

        def runs(i):
            dst = grouped[i][:].rearrange("p (c r) j -> p c j r", r=RUN)
            src = raw[i][:].rearrange("p j (c r) -> p c j r", r=RUN)
            return dst, src, shares(i)[0] // RUN, sum(shares(i)) // RUN

        def vector_regroup(i):
            if i < PIECES and shares(i)[2]:
                dst, src, first, cut = runs(i)
                nc.vector.tensor_copy(out=dst[:, first:cut], in_=src[:, first:cut])

        def scalar_regroup(i):
            if i >= PIECES:
                return
            nc.scalar.copy(out=grouped[i][:, : shares(i)[0], :], in_=passed[i][:])
            dst, src, first, cut = runs(i)
            if shares(i)[1]:
                cut -= 1
            if cut < COLS // RUN:
                nc.scalar.copy(out=dst[:, cut:], in_=src[:, cut:])
            load(i + RAW_BUFS)

        def quantise(i):
            if i >= PIECES:
                return
            codes[i] = packed.tile([P, COLS], U32, name="codes", align_bytes=64)
            scales[i] = packed.tile([P, COLS], U8, name="scales", align_bytes=64)
            nc.vector.quantize_mx(
                out=codes[i][:].bitcast(FP8X4),
                scales=scales[i][:],
                in_=grouped[i][:].rearrange("p w j -> p (w j)"),
            )

        def load_weight(w, label):
            w_sb = const.tile([P, PACK, H], BF16, name=label + "_sb")
            nc.sync.dma_start(out=w_sb[:], in_=w.rearrange("(q t) h -> q t h", t=PACK))
            w_codes = const.tile([P, PACK, P], U32, name=label + "_codes", align_bytes=64)
            w_scales = const.tile([P, PACK, P], U8, name=label + "_scales", align_bytes=64)
            return w_sb, w_codes, w_scales

        def turn_weight(weight, t, count):
            turned = banks.tile([P, count, 2, P], F32, name="turned", tag="x3")
            for k in range(count):
                words = weight[0][:, t + k, :].bitcast(F32).rearrange("q (p u) -> q u p", u=2)
                for u in range(2):
                    nc.tensor.transpose(turned[:, k, u, :], words[:, u, :], identity[:])
            w_grouped[t] = work.tile([P, count * H], BF16, name="w_grouped", align_bytes=64)
            nc.scalar.copy(
                out=w_grouped[t][:].bitcast(F32).rearrange("p (k q u) -> p k q u", k=count, u=2),
                in_=turned[:].rearrange("p k u q -> p k q u"),
            )

        def pack_weight(weight, t, count):
            nc.vector.quantize_mx(
                out=weight[1][:, t : t + count, :].rearrange("p k q -> p (k q)").bitcast(FP8X4),
                scales=weight[2][:, t : t + count, :].rearrange("p k q -> p (k q)"),
                in_=w_grouped[t][:],
            )

        def multiply(i):
            for t in scalar_tiles(i) + vector_tiles(i):
                x3[i, t] = banks.tile([P, COLS], F32, name="x3")
                nc.tensor.matmul_mx(
                    out=x3[i, t][:],
                    lhsT=w3[1][:, t, :].bitcast(FP8X4),
                    lhsT_scale=w3[2][:, t, :],
                    rhs=codes[i][:].bitcast(FP8X4),
                    rhs_scale=scales[i][:],
                    start=True,
                    stop=True,
                )

        def pool_raw(i):
            for t in vector_tiles(i):
                if i == 0:
                    nc.vector.tensor_scalar_mul(out=best_raw[:, t, :], in0=x3[i, t][:], scalar1=gain1[:, t : t + 1])
                else:
                    nc.vector.scalar_tensor_tensor(
                        out=best_raw[:, t, :],
                        in0=x3[i, t][:],
                        scalar=gain1[:, t : t + 1],
                        in1=best_raw[:, t, :],
                        op0=ALU.mult,
                        op1=ALU.max,
                    )

        def norm_relu(dst, src, t, gain):
            nc.scalar.activation(out=dst, in_=src, func=RELU, bias=shift1[:, t : t + 1], scale=gain)

        def activate(i):
            if i > 0:
                h3[i] = work.tile([P, PACK - 1, COLS], BF16, name="h3")
            for t in scalar_tiles(i):
                if i == LATE and t in vector_tiles(0):
                    norm_relu(best[:, t, :], best_raw[:, t, :], t, 1.0)
                norm_relu(best[:, t, :] if i == 0 else h3[i][:, t - 1, :], x3[i, t][:], t, gain1[:, t : t + 1])

        def merge(i):
            if i >= 1:
                low = min(scalar_tiles(i))
                nc.vector.tensor_max(out=best[:, low:, :], in0=best[:, low:, :], in1=h3[i][:, low - 1 :, :])

        def load_batch_norm(queue, g, b, m, v, label):
            loaded = const.tile([P, 4, 16], BF16, name=label + "_loaded")
            for slot, vec in enumerate((g, b, m, v)):
                queue.dma_start(out=loaded[:, slot, 0:PACK], in_=vec.rearrange("(q t) -> q t", t=PACK))
            return loaded

        def start_batch_norm(loaded, label):
            spread = const.tile([P, PACK], F32, name=label + "_spread")
            nc.vector.tensor_scalar_add(out=spread[:], in0=loaded[:, 3, 0:PACK], scalar1=BN_EPS)
            nc.scalar.sqrt(out=spread[:], in_=spread[:])
            return spread

        def finish_batch_norm(loaded, spread, label):
            gain = const.tile([P, PACK], F32, name=label + "_gain")
            offset = const.tile([P, PACK], F32, name=label + "_offset")
            shift = const.tile([P, PACK], F32, name=label + "_shift")
            return gain, shift, (
                lambda: nc.vector.reciprocal(out=spread[:], in_=spread[:]),
                lambda: nc.vector.tensor_mul(out=gain[:], in0=loaded[:, 0, 0:PACK], in1=spread[:]),
                lambda: nc.vector.tensor_mul(out=offset[:], in0=gain[:], in1=loaded[:, 2, 0:PACK]),
                lambda: nc.vector.tensor_sub(out=shift[:], in0=loaded[:, 1, 0:PACK], in1=offset[:]),
            )

        def gpsimd_batch_norm(loaded, label):
            spread = const.tile([P, PACK], F32, name=label + "_spread")
            gain = const.tile([P, PACK], F32, name=label + "_gain")
            offset = const.tile([P, PACK], F32, name=label + "_offset")
            shift = const.tile([P, PACK], F32, name=label + "_shift")
            nc.gpsimd.tensor_scalar(
                out=spread[:], in0=loaded[:, 3, 0:PACK], scalar1=1.0, scalar2=BN_EPS, op0=ALU.mult, op1=ALU.add
            )
            nc.gpsimd.tensor_tensor(out=spread[:], in0=spread[:], in1=minus_half[:], op=ALU.pow)
            nc.gpsimd.tensor_tensor(out=gain[:], in0=loaded[:, 0, 0:PACK], in1=spread[:], op=ALU.mult)
            nc.gpsimd.tensor_tensor(out=offset[:], in0=gain[:], in1=loaded[:, 2, 0:PACK], op=ALU.mult)
            nc.gpsimd.tensor_tensor(out=shift[:], in0=loaded[:, 1, 0:PACK], in1=offset[:], op=ALU.subtract)
            return gain, shift

        load(0)
        w3 = load_weight(W3, "w3")
        bn1_loaded = load_batch_norm(nc.sync, g3, b3, m3, v3, "bn1")
        for i in range(1, RAW_BUFS):
            load(i)

        warm = const.tile([P, 1], F32, name="warm")
        nc.vector.memset(warm[:], 1.0)
        nc.scalar.sqrt(out=warm[:], in_=warm[:])
        minus_half = const.tile([P, PACK], F32, name="minus_half")
        nc.vector.memset(minus_half[:], -0.5)
        identity_bf = const.tile([P, P], BF16, name="identity_bf")
        make_identity(nc, identity_bf[:])
        identity = const.tile([P, P], F32, name="identity")
        make_identity(nc, identity[:])
        best_raw = const.tile([P, len(vector_tiles(0)), COLS], F32, name="best_raw")
        best = const.tile([P, PACK, COLS], BF16, name="best")

        def regroup(i):
            start_regroup(i)
            vector_regroup(i)
            scalar_regroup(i)

        regroup(0)
        quantise(0)
        first_tiles = scalar_tiles(0) + vector_tiles(0)
        for t in first_tiles[:2]:
            turn_weight(w3, t, 1)
        spread1 = start_batch_norm(bn1_loaded, "bn1")
        gain1, shift1, bn1_steps = finish_batch_norm(bn1_loaded, spread1, "bn1")
        for t in first_tiles[2:]:
            turn_weight(w3, t, 1)
        for t in first_tiles[:2]:
            pack_weight(w3, t, 1)
        for t, step in zip(first_tiles[2:], bn1_steps):
            step()
            pack_weight(w3, t, 1)
        for i in range(1, AHEAD):
            regroup(i)
            bn1_steps[i + 1]()
        multiply(0)
        wc = load_weight(Wc1, "wc")
        bn2_loaded = load_batch_norm(nc.sync, gc1, bc1, mc1, vc1, "bn2")

        for i in range(PIECES):
            if i > 0:
                multiply(i)
            quantise(i + 1)
            start_regroup(i + AHEAD)
            merge(i - MERGE_LAG)
            vector_regroup(i + AHEAD)
            pool_raw(i)
            activate(i)
            scalar_regroup(i + AHEAD)
            if i in (WC_FROM + 1, WC_FROM + 2):
                pack_weight(wc, 2 * (i - WC_FROM - 1), 2)
            if i in (WC_FROM, WC_FROM + 1):
                turn_weight(wc, 2 * (i - WC_FROM), 2)

        gain2, shift2 = gpsimd_batch_norm(bn2_loaded, "bn2")

        for t in vector_tiles(PIECES - 1):
            norm_relu(best[:, t, :], best_raw[:, t, :], t, 1.0)
        for i in range(PIECES - MERGE_LAG, PIECES):
            merge(i)
        half = const.tile([P, PACK, 2 * N_SEARCH], BF16, name="half")
        nc.vector.tensor_max(out=half[:], in0=best[:, :, : 2 * N_SEARCH], in1=best[:, :, 2 * N_SEARCH :])
        pooled = const.tile([P, N_SEARCH, PACK], BF16, name="pooled", align_bytes=64)
        nc.vector.tensor_max(
            out=pooled[:],
            in0=half[:, :, :N_SEARCH].rearrange("p t n -> p n t"),
            in1=half[:, :, N_SEARCH:].rearrange("p t n -> p n t"),
        )
        p_codes = const.tile([P, N_SEARCH], U32, name="p_codes", align_bytes=64)
        p_scales = const.tile([P, N_SEARCH], U8, name="p_scales", align_bytes=64)
        nc.vector.quantize_mx(
            out=p_codes[:].bitcast(FP8X4), scales=p_scales[:], in_=pooled[:].rearrange("p n t -> p (n t)")
        )
        result = const.tile([P, PACK, N_SEARCH], F32, name="result")
        for t in range(PACK):
            xc = banks.tile([P, N_SEARCH], F32, name="xc", tag="x3")
            nc.tensor.matmul_mx(
                out=xc[:],
                lhsT=wc[1][:, t, :].bitcast(FP8X4),
                lhsT_scale=wc[2][:, t, :],
                rhs=p_codes[:].bitcast(FP8X4),
                rhs_scale=p_scales[:],
                start=True,
                stop=True,
            )
            nc.scalar.activation(
                out=result[:, t, :], in_=xc[:], func=RELU, bias=shift2[:, t : t + 1], scale=gain2[:, t : t + 1]
            )
            if t % 2 == 1:
                nc.sync.dma_start(
                    out=out[0].rearrange("(q t) n -> q t n", t=PACK)[:, t - 1 : t + 1, :], in_=result[:, t - 1 : t + 1, :]
                )
